import numpy as np
import ml_dtypes


def mxq(x, axis, fmt="e4m3"):
    dtype, down = {"e4m3": (ml_dtypes.float8_e4m3fn, 7), "e5m2": (ml_dtypes.float8_e5m2, 14)}[fmt]
    v = np.moveaxis(np.asarray(x, np.float32).astype(ml_dtypes.bfloat16).astype(np.float64), axis, -1)
    blocks = v.reshape(v.shape[:-1] + (-1, 32))
    amax = np.abs(blocks).max(-1, keepdims=True)
    byte = np.maximum(np.where(amax > 0, np.frexp(amax)[1] - 1 + 127, 0) - down, 1)
    scale = np.exp2(byte - 127.0)
    codes = (blocks / scale).astype(np.float32).astype(dtype).astype(np.float64)
    return np.moveaxis((codes * scale).reshape(v.shape), -1, axis)


WIDE = False


def mx_kscale(k):
    if not WIDE:
        return np.ones(k)
    levels = np.array([10, -10, 5, -5, 0])
    if k % 512:
        return np.exp2(np.random.permutation(np.resize(levels, k // 32))).repeat(32)
    a = np.empty((k // 512, 16))
    for p in range(k // 512):
        a[p, :8] = np.random.permutation(np.resize(levels, 8))
        for g in range(8):
            far = levels[np.abs(levels - a[p, g]) >= 10]
            a[p, g + 8] = far[np.random.randint(len(far))]
    return np.exp2(a.ravel()).repeat(32)


BF16 = ml_dtypes.bfloat16


def bf(x):
    return np.asarray(x, np.float32).astype(BF16)


def f64(x):
    return np.asarray(x).astype(np.float64)


B, C, H, W, K, HID, LAT = 4, 512, 16, 16, 8, 512, 32
REDUCTION = -0.1
CLAMP = 500.0
HOT = 1.2 * CLAMP / (-REDUCTION * C * np.sqrt(2.0 / np.pi))


def draw0():
    s = mx_kscale(HID)
    amp = np.where(np.random.random((B, 1, H, W)) < 0.125, HOT, 1.0)
    return {"d": bf(np.tanh(np.random.standard_normal((K, B, HID, H, W))) * s[:, None, None]),
            "W_dec": bf(np.random.standard_normal((K, C, HID)) * 1.1 / np.sqrt(HID) / s),
            "x": bf(np.random.standard_normal((B, C, H, W)) * amp)}


def core(d, W_dec, x):
    xf = f64(x)
    wq = mxq(f64(W_dec), 2, "e4m3")
    dq = mxq(f64(d), 2, "e4m3")
    recon = (wq[:, None] @ dq.reshape(K, B, HID, H * W)).reshape(K, B, C, H, W)
    err = np.sum(np.abs(recon - xf[None]), axis=2) * REDUCTION
    logits = np.swapaxes(np.clip(err, -CLAMP, CLAMP), 0, 1)
    e = np.exp(logits - logits.max(axis=1, keepdims=True))
    p = e / e.sum(axis=1, keepdims=True)
    error = np.mean(logits, axis=(2, 3))
    return p, error, np.swapaxes(recon, 0, 1)


def e4m3fn_bytes(y):
    return np.clip(np.asarray(y, np.float64), -448.0, 448.0).astype(np.float32).astype(ml_dtypes.float8_e4m3fn).view(np.uint8)


def e4m3fn_values(b):
    return np.asarray(b, np.uint8).view(ml_dtypes.float8_e4m3fn).astype(np.float64)


def setup_inputs():
    d = draw0()
    x0 = np.asarray(d['d']).astype(np.float64)
    s = (np.max(np.abs(x0), axis=(0, 1, 3, 4), keepdims=True) / 448.0).astype(np.float32)
    out = {}
    for k, v in d.items():
        if k == 'd':
            out['d_bytes'] = e4m3fn_bytes(x0 / s.astype(np.float64))
            out['d_scale'] = s
        else:
            out[k] = v
    return out


def reference(d_bytes, d_scale, W_dec, x):
    return core(e4m3fn_values(d_bytes) * d_scale.astype(np.float64), W_dec, x)

@@ -1,0 +1,332 @@
+from contextlib import ExitStack
+
+import concourse.mybir as mybir
+from concourse.masks import make_identity
+
+F32 = mybir.dt.float32
+BF16 = mybir.dt.bfloat16
+U32 = mybir.dt.uint32
+U8 = mybir.dt.uint8
+FP8 = mybir.dt.float8_e4m3fn
+FP8X4 = mybir.dt.float8_e4m3fn_x4
+ALU = mybir.AluOpType
+ACT = mybir.ActivationFunctionType
+AX = mybir.AxisListType
+
+NCLS, NIMG, CH, HID, POS = 8, 4, 512, 512, 256
+P = 128
+NSTEP = 2 * NCLS
+FLOPS = 2 * NCLS * NIMG * CH * HID * POS
+
+GP_INTERLEAVE = False
+
+
+def tile_cssrclassifier_pa_kernel(tc, d_bytes, d_scale, W_dec, x, out_0, out_1, out_2):
+    nc = tc.nc
+    with ExitStack() as ctx:
+        keep = ctx.enter_context(tc.tile_pool(name="keep", bufs=1))
+        work = ctx.enter_context(tc.tile_pool(name="work", bufs=2))
+        psum = ctx.enter_context(tc.psum_pool(name="psum", bufs=2))
+        ctx.enter_context(tc.manual_schedule())
+
+        sc = keep.tile([P, 4], F32, name="sc")
+        dbytes = [keep.tile([P, NIMG, 1024], U8, name="dbytes%d" % k) for k in range(NCLS)]
+        wraw = [keep.tile([P, 4, HID], BF16, name="wraw%d" % k) for k in range(NCLS)]
+        xraw = keep.tile([P, NIMG, 4, POS], BF16, name="xraw")
+        xT = keep.tile([P, 8, CH], BF16, name="xT")
+        ident_f = keep.tile([P, P], F32, name="ident_f")
+        ident_b = keep.tile([P, P], BF16, name="ident_b")
+        ones_b = keep.tile([P, 2], BF16, name="ones_b")
+        zer = keep.tile([P, 1], F32, name="zer")
+        warm = keep.tile([P, 1], F32, name="warm")
+        sel = keep.tile([P, NIMG, P], F32, name="sel")
+        msum = keep.tile([P, 64], F32, name="msum")
+        asum = keep.tile([P, 64], F32, name="asum")
+        x01 = keep.tile([P, 8], F32, name="x01")
+        pmat = keep.tile([P, P], F32, name="pmat")
+
+        def load_d(k, b0, b1):
+            nc.sync.dma_start(
+                out=dbytes[k][:, b0:b1, :],
+                in_=d_bytes[k, b0:b1].rearrange("b (p t) y z -> p b (t y z)", t=4),
+            )
+
+        def load_w(k):
+            nc.sync.dma_start(
+                out=wraw[k][:].rearrange("p i j -> p (i j)"),
+                in_=W_dec[k].rearrange("(m i) j -> m (i j)", i=4),
+            )
+
+        def load_x(b0, b1):
+            nc.sync.dma_start(
+                out=xraw[:, b0:b1].rearrange("p b i n -> p b (i n)"),
+                in_=x[b0:b1].rearrange("b (m i) y z -> m b (i y z)", i=4),
+            )
+
+        nc.sync.dma_start(out=sc[:], in_=d_scale[0, 0, :, 0, 0].rearrange("(p t) -> p t", t=4))
+        load_d(0, 0, 2)
+        load_w(0)
+        load_d(0, 2, 4)
+        load_x(0, 2)
+        load_d(1, 0, 4)
+        load_x(2, 4)
+        load_w(1)
+        for k in range(2, NCLS):
+            load_d(k, 0, 4)
+            load_w(k)
+
+        nc.gpsimd.memset(zer[:], 0.0)
+        make_identity(nc, ident_f[:])
+        make_identity(nc, ident_b[:])
+        nc.gpsimd.memset(ones_b[:], 1.0)
+        nc.gpsimd.memset(sel[:], 0.0)
+        for b in range(NIMG):
+            nc.gpsimd.memset(sel[:, b, b:b + 1], 1.0 / POS)
+        nc.gpsimd.memset(pmat[:], 0.0)
+        nc.scalar.activation(out=warm[:], in_=zer[:], func=ACT.Exp)
+
+        wide, grp, dq, dsc = {}, {}, {}, {}
+        wtp, wgrp, wq, wsc = {}, {}, {}, {}
+        xtp, rst, ppt, qqt, qst = {}, {}, {}, {}, {}
+
+        def widen(s, lo, hi):
+            k, h = divmod(s, 2)
+            if lo == 0:
+                wide[s] = work.tile([P, 4, 512], BF16, name="wide", tag="wide", bufs=3)
+            for idx in range(lo, hi):
+                b2, t = divmod(idx, 4)
+                nc.scalar.activation(
+                    out=wide[s][:, t, b2 * POS:(b2 + 1) * POS],
+                    in_=dbytes[k][:, 2 * h + b2, t * POS:(t + 1) * POS].bitcast(FP8),
+                    func=ACT.Copy,
+                    scale=sc[:, t:t + 1],
+                )
+
+        def interleave(s, b2):
+            if b2 == 0:
+                grp[s] = work.tile([P, 512, 4], BF16, name="grp", tag="grp", bufs=2, align_bytes=64)
+            dst = grp[s][:, b2 * POS:(b2 + 1) * POS, :]
+            src = wide[s][:, :, b2 * POS:(b2 + 1) * POS].rearrange("p t c -> p c t")
+            if GP_INTERLEAVE:
+                nc.gpsimd.tensor_scalar(out=dst, in0=src, scalar1=1.0, scalar2=0.0, op0=ALU.mult, op1=ALU.add)
+            else:
+                nc.vector.tensor_copy(out=dst, in_=src)
+
+        def quant_d(s):
+            dq[s] = work.tile([P, 512], U32, name="dq", tag="dq", bufs=3, align_bytes=64)
+            dsc[s] = work.tile([P, 512], U8, name="dsc", tag="dsc", bufs=3, align_bytes=64)
+            nc.vector.quantize_mx(
+                out=dq[s][:].bitcast(FP8X4),
+                scales=dsc[s][:],
+                in_=grp[s][:].rearrange("p c t -> p (c t)"),
+            )
+
+        def wtrans(k):
+            for ii in range(2):
+                tp = psum.tile([P, 2, 2, P], F32, name="wtp", tag="tt")
+                wtp[(k, ii)] = tp
+                for i2 in range(2):
+                    words = wraw[k][:, 2 * ii + i2, :].bitcast(F32)
+                    for u in range(2):
+                        nc.tensor.transpose(tp[:, i2, u, :], words[:, u:256:2], ident_f[:])
+
+        def wevac(k, ii, eng):
+            if ii == 0:
+                wgrp[k] = work.tile([P, 512, 4], BF16, name="wgrp", tag="wgrp", bufs=2, align_bytes=64)
+            flat = wgrp[k][:].rearrange("p c t -> p (c t)").bitcast(F32)
+            dst = flat[:, ii * 512:(ii + 1) * 512].rearrange("p (i m u) -> p i m u", i=2, u=2)
+            src = wtp[(k, ii)][:].rearrange("p i u m -> p i m u")
+            if eng == "v":
+                nc.vector.tensor_copy(out=dst, in_=src)
+            else:
+                nc.scalar.copy(out=dst, in_=src)
+
+        def quant_w(k):
+            wq[k] = work.tile([P, 512], U32, name="wq", tag="wq", bufs=2, align_bytes=64)
+            wsc[k] = work.tile([P, 512], U8, name="wsc", tag="wsc", bufs=2, align_bytes=64)
+            nc.vector.quantize_mx(
+                out=wq[k][:].bitcast(FP8X4),
+                scales=wsc[k][:],
+                in_=wgrp[k][:].rearrange("p c t -> p (c t)"),
+            )
+
+        def xtrans(u, tag):
+            b, f = divmod(u, 2)
+            xp = psum.tile([P, 4, P], BF16, name="xtp", tag=tag)
+            xtp[u] = xp
+            for i in range(4):
+                nc.tensor.transpose(xp[:, i, :], xraw[:, b, i, f * P:(f + 1) * P], ident_b[:])
+
+        def xevac(u):
+            nc.scalar.copy(out=xT[:, u, :], in_=xtp[u][:].rearrange("p i m -> p (i m)"))
+
+        def mm_p(s, i):
+            k = s // 2
+            pp = psum.tile([P, 512], F32, name="pp", tag="pp")
+            ppt[(s, i)] = pp
+            cols = slice(i * P, (i + 1) * P)
+            nc.tensor.matmul_mx(
+                out=pp[:],
+                lhsT=wq[k][:, cols].bitcast(FP8X4), lhsT_scale=wsc[k][:, cols],
+                rhs=dq[s][:].bitcast(FP8X4), rhs_scale=dsc[s][:],
+                start=True, stop=True,
+            )
+
+        def rcopy(s, i):
+            if i == 0:
+                rst[s] = work.tile([P, 2, 4, POS], F32, name="rst", tag="rst", bufs=3)
+            nc.scalar.copy(out=rst[s][:, :, i, :], in_=ppt[(s, i)][:].rearrange("p (b n) -> p b n", b=2))
+
+        def store(s):
+            k, h = divmod(s, 2)
+            nc.sync.dma_start(
+                out=out_2[2 * h:2 * h + 2, k].rearrange("b (m i) y z -> m b (i y z)", i=4),
+                in_=rst[s][:].rearrange("p b i n -> p b (i n)"),
+            )
+
+        def mm_q(s, v):
+            k = s // 2
+            qq = psum.tile([P, 512], F32, name="qq", tag="qq")
+            qqt[(s, v)] = qq
+            cols = slice(v * P, (v + 1) * P)
+            nc.tensor.matmul_mx(
+                out=qq[:],
+                lhsT=dq[s][:, cols].bitcast(FP8X4), lhsT_scale=dsc[s][:, cols],
+                rhs=wq[k][:].bitcast(FP8X4), rhs_scale=wsc[k][:],
+                start=True, stop=True,
+            )
+
+        def mm_qs(s, v):
+            k = s // 2
+            if v == 0:
+                qst[s] = psum.tile([P, 4, P], F32, name="qs", tag="qs")
+            cols = slice(v * P, (v + 1) * P)
+            for i in range(4):
+                wc = slice(i * P, (i + 1) * P)
+                nc.tensor.matmul_mx(
+                    out=qst[s][:, v, :],
+                    lhsT=dq[s][:, cols].bitcast(FP8X4), lhsT_scale=dsc[s][:, cols],
+                    rhs=wq[k][:, wc].bitcast(FP8X4), rhs_scale=wsc[k][:, wc],
+                    start=(i == 0), stop=(i == 3),
+                )
+
+        def stt(s, v):
+            h = s % 2
+            junk = work.tile([P, 512], F32, name="junk", tag="junk", bufs=2)
+            nc.vector.scalar_tensor_tensor(
+                out=junk[:], in0=qqt[(s, v)][:], scalar=1.0, in1=xT[:, 4 * h + v, :],
+                op0=ALU.mult, op1=ALU.max, accum_out=msum[:, 4 * s + v:4 * s + v + 1],
+            )
+
+        def red(s):
+            nc.vector.tensor_reduce(out=asum[:, 4 * s:4 * s + 4], in_=qst[s][:], axis=AX.X, op=ALU.add)
+
+        widen(0, 0, 8)
+        wtrans(0)
+        interleave(0, 0)
+        wevac(0, 0, "v")
+        interleave(0, 1)
+        wevac(0, 1, "v")
+        quant_d(0)
+        quant_w(0)
+        xtrans(0, "qq")
+        xtrans(1, "qq")
+        xtrans(2, "qs")
+        xtrans(3, "qs")
+        widen(1, 0, 4)
+        xevac(0)
+        xevac(1)
+        widen(1, 4, 8)
+        xevac(2)
+        xevac(3)
+
+        xs = None
+        for s in range(NSTEP):
+            k, h = divmod(s, 2)
+            for q in range(4):
+                mm_p(s, q)
+                mm_q(s, q)
+                mm_qs(s, q)
+                if s == 0 and q in (0, 2):
+                    xtrans(4 + q, "tt")
+                    xtrans(5 + q, "tt")
+                if h == 1 and q == 0 and k + 1 < NCLS:
+                    wtrans(k + 1)
+                if s == NSTEP - 2:
+                    if q == 0:
+                        xs = psum.tile([P, 8], F32, name="xs", tag="tt")
+                    for u in (2 * q, 2 * q + 1):
+                        b, f = divmod(u, 2)
+                        for i in range(4):
+                            nc.tensor.matmul(
+                                out=xs[:, u:u + 1], lhsT=xraw[:, b, i, f * P:(f + 1) * P], rhs=ones_b[:, 0:1],
+                                start=(i == 0), stop=(i == 3),
+                            )
+
+                if s + 2 < NSTEP:
+                    widen(s + 2, 2 * q, 2 * q + 2)
+                rcopy(s, q)
+                if s == 0 and q in (1, 3):
+                    xevac(3 + q)
+                    xevac(4 + q)
+                if h == 1 and q in (1, 2) and k + 1 < NCLS:
+                    wevac(k + 1, q - 1, "s")
+                if q == 3:
+                    store(s)
+
+                if s + 1 < NSTEP:
+                    if q < 2:
+                        interleave(s + 1, q)
+                    elif q == 2:
+                        quant_d(s + 1)
+                if h == 1 and q == 3 and k + 1 < NCLS:
+                    quant_w(k + 1)
+                stt(s, q)
+                if q == 3:
+                    red(s)
+                    if s == NSTEP - 2:
+                        nc.vector.tensor_scalar(out=x01[:], in0=xs[:], scalar1=0.1, scalar2=None, op0=ALU.mult)
+
+        t1 = keep.tile([P, 64], F32, name="t1")
+        nc.vector.scalar_tensor_tensor(out=t1[:], in0=msum[:], scalar=2.0, in1=asum[:], op0=ALU.mult, op1=ALU.subtract)
+        lg0 = keep.tile([P, 64], F32, name="lg0")
+        nc.vector.scalar_tensor_tensor(
+            out=lg0[:].rearrange("p (k u) -> p k u", k=8), in0=t1[:].rearrange("p (k u) -> p k u", k=8), scalar=-0.1,
+            in1=x01[:].rearrange("p (o u) -> p o u", o=1).to_broadcast([P, 8, 8]), op0=ALU.mult, op1=ALU.add,
+        )
+        lg = keep.tile([P, 64], F32, name="lg")
+        nc.vector.tensor_scalar(out=lg[:], in0=lg0[:], scalar1=-500.0, scalar2=500.0, op0=ALU.max, op1=ALU.min)
+        mx = keep.tile([P, 8], F32, name="mx")
+        nc.vector.tensor_reduce(out=mx[:], in_=lg[:].rearrange("p (k u) -> p u k", k=8), axis=AX.X, op=ALU.max)
+        sh = keep.tile([P, 64], F32, name="sh")
+        nc.vector.tensor_tensor(
+            out=sh[:].rearrange("p (k u) -> p k u", k=8), in0=lg[:].rearrange("p (k u) -> p k u", k=8),
+            in1=mx[:].rearrange("p (o u) -> p o u", o=1).to_broadcast([P, 8, 8]), op=ALU.subtract,
+        )
+        ex = keep.tile([P, 64], F32, name="ex")
+        nc.scalar.activation(out=ex[:], in_=sh[:], func=ACT.Exp)
+        lsum = keep.tile([P, 32], F32, name="lsum")
+        lg4 = lg[:].rearrange("p (k b f) -> p k b f", k=8, b=4)
+        nc.vector.tensor_tensor(
+            out=lsum[:].rearrange("p (b k) -> p k b", b=4), in0=lg4[:, :, :, 0], in1=lg4[:, :, :, 1], op=ALU.add,
+        )
+        er = psum.tile([P, 8], F32, name="er", tag="tt")
+        for b in range(NIMG):
+            nc.tensor.matmul(out=er[:], lhsT=sel[:, b, :], rhs=lsum[:, b * 8:(b + 1) * 8], start=(b == 0), stop=(b == NIMG - 1))
+        ers = keep.tile([P, 8], F32, name="ers")
+        nc.scalar.copy(out=ers[:], in_=er[:])
+        nc.sync.dma_start(out=out_1, in_=ers[0:4, :])
+        sm = keep.tile([P, 8], F32, name="sm")
+        nc.vector.tensor_reduce(out=sm[:], in_=ex[:].rearrange("p (k u) -> p u k", k=8), axis=AX.X, op=ALU.add)
+        rs = keep.tile([P, 8], F32, name="rs")
+        nc.vector.reciprocal(out=rs[:], in_=sm[:])
+        nc.vector.tensor_tensor(
+            out=pmat[:, 0:64].rearrange("p (b k f) -> p k b f", b=4, k=8),
+            in0=ex[:].rearrange("p (k b f) -> p k b f", k=8, b=4),
+            in1=rs[:].rearrange("p (o b f) -> p o b f", o=1, b=4).to_broadcast([P, 8, 4, 2]), op=ALU.mult,
+        )
+        ptp = psum.tile([P, P], F32, name="ptp", tag="tt")
+        nc.tensor.transpose(ptp[:], pmat[:], ident_f[:])
+        pts = keep.tile([P, P], F32, name="pts")
+        nc.vector.tensor_copy(out=pts[:], in_=ptp[:])
+        nc.sync.dma_start(out=out_0.rearrange("b k (f g) w -> (b k f) (g w)", f=2), in_=pts[0:64, :])

@@ -18,7 +18,7 @@ P = 128
 NSTEP = 2 * NCLS
 FLOPS = 2 * NCLS * NIMG * CH * HID * POS
 
-GP_INTERLEAVE = False
+RC_ON_VECTOR = (3,)
 
 
 def tile_cssrclassifier_pa_kernel(tc, d_bytes, d_scale, W_dec, x, out_0, out_1, out_2):
@@ -102,12 +102,12 @@ def tile_cssrclassifier_pa_kernel(tc, d_bytes, d_scale, W_dec, x, out_0, out_1, 
                     scale=sc[:, t:t + 1],
                 )
 
-        def interleave(s, b2):
+        def interleave(s, b2, eng):
             if b2 == 0:
-                grp[s] = work.tile([P, 512, 4], BF16, name="grp", tag="grp", bufs=2, align_bytes=64)
+                grp[s] = work.tile([P, 512, 4], BF16, name="grp", tag="grp", bufs=1, align_bytes=64)
             dst = grp[s][:, b2 * POS:(b2 + 1) * POS, :]
             src = wide[s][:, :, b2 * POS:(b2 + 1) * POS].rearrange("p t c -> p c t")
-            if GP_INTERLEAVE:
+            if eng == "g":
                 nc.gpsimd.tensor_scalar(out=dst, in0=src, scalar1=1.0, scalar2=0.0, op0=ALU.mult, op1=ALU.add)
             else:
                 nc.vector.tensor_copy(out=dst, in_=src)
@@ -172,10 +172,13 @@ def tile_cssrclassifier_pa_kernel(tc, d_bytes, d_scale, W_dec, x, out_0, out_1, 
                 start=True, stop=True,
             )
 
-        def rcopy(s, i):
+        def rcopy(s, i, eng):
             if i == 0:
                 rst[s] = work.tile([P, 2, 4, POS], F32, name="rst", tag="rst", bufs=3)
-            nc.scalar.copy(out=rst[s][:, :, i, :], in_=ppt[(s, i)][:].rearrange("p (b n) -> p b n", b=2))
+            if eng == "v":
+                nc.vector.tensor_copy(out=rst[s][:, :, i, :], in_=ppt[(s, i)][:].rearrange("p (b n) -> p b n", b=2))
+            else:
+                nc.scalar.copy(out=rst[s][:, :, i, :], in_=ppt[(s, i)][:].rearrange("p (b n) -> p b n", b=2))
 
         def store(s):
             k, h = divmod(s, 2)
@@ -223,9 +226,9 @@ def tile_cssrclassifier_pa_kernel(tc, d_bytes, d_scale, W_dec, x, out_0, out_1, 
 
         widen(0, 0, 8)
         wtrans(0)
-        interleave(0, 0)
+        interleave(0, 0, "v")
         wevac(0, 0, "v")
-        interleave(0, 1)
+        interleave(0, 1, "v")
         wevac(0, 1, "v")
         quant_d(0)
         quant_w(0)
@@ -239,10 +242,13 @@ def tile_cssrclassifier_pa_kernel(tc, d_bytes, d_scale, W_dec, x, out_0, out_1, 
         widen(1, 4, 8)
         xevac(2)
         xevac(3)
+        interleave(1, 0, "g")
+        interleave(1, 1, "g")
 
         xs = None
         for s in range(NSTEP):
             k, h = divmod(s, 2)
+            more_w = k + 1 < NCLS
             for q in range(4):
                 mm_p(s, q)
                 mm_q(s, q)
@@ -250,7 +256,7 @@ def tile_cssrclassifier_pa_kernel(tc, d_bytes, d_scale, W_dec, x, out_0, out_1, 
                 if s == 0 and q in (0, 2):
                     xtrans(4 + q, "tt")
                     xtrans(5 + q, "tt")
-                if h == 1 and q == 0 and k + 1 < NCLS:
+                if more_w and ((k == 0 and h == 1 and q == 0) or (k > 0 and h == 0 and q == 2)):
                     wtrans(k + 1)
                 if s == NSTEP - 2:
                     if q == 0:
@@ -262,30 +268,37 @@ def tile_cssrclassifier_pa_kernel(tc, d_bytes, d_scale, W_dec, x, out_0, out_1, 
                                 out=xs[:, u:u + 1], lhsT=xraw[:, b, i, f * P:(f + 1) * P], rhs=ones_b[:, 0:1],
                                 start=(i == 0), stop=(i == 3),
                             )
-
                 if s + 2 < NSTEP:
                     widen(s + 2, 2 * q, 2 * q + 2)
-                rcopy(s, q)
+                on_v = q in RC_ON_VECTOR and s + 2 < NSTEP
+                if not on_v:
+                    rcopy(s, q, "s")
                 if s == 0 and q in (1, 3):
                     xevac(3 + q)
                     xevac(4 + q)
-                if h == 1 and q in (1, 2) and k + 1 < NCLS:
+                if more_w and k == 0 and h == 1 and q in (1, 2):
                     wevac(k + 1, q - 1, "s")
-                if q == 3:
-                    store(s)
-
-                if s + 1 < NSTEP:
-                    if q < 2:
-                        interleave(s + 1, q)
-                    elif q == 2:
+                if more_w and k > 0 and h == 0 and q == 3:
+                    wevac(k + 1, 0, "s")
+                if more_w and k > 0 and h == 1 and q == 0:
+                    wevac(k + 1, 1, "s")
+                if q == 2:
+                    if more_w and k > 0 and h == 1:
+                        quant_w(k + 1)
+                    if s + 1 < NSTEP:
                         quant_d(s + 1)
-                if h == 1 and q == 3 and k + 1 < NCLS:
+                if more_w and k == 0 and h == 1 and q == 3:
                     quant_w(k + 1)
                 stt(s, q)
+                if on_v:
+                    rcopy(s, q, "v")
                 if q == 3:
                     red(s)
                     if s == NSTEP - 2:
                         nc.vector.tensor_scalar(out=x01[:], in0=xs[:], scalar1=0.1, scalar2=None, op0=ALU.mult)
+                    store(s)
+                if s + 2 < NSTEP and q >= 2:
+                    interleave(s + 2, q - 2, "g")
 
         t1 = keep.tile([P, 64], F32, name="t1")
         nc.vector.scalar_tensor_tensor(out=t1[:], in0=msum[:], scalar=2.0, in1=asum[:], op0=ALU.mult, op1=ALU.subtract)

@@ -18,8 +18,6 @@ P = 128
 NSTEP = 2 * NCLS
 FLOPS = 2 * NCLS * NIMG * CH * HID * POS
 
-RC_ON_VECTOR = (3,)
-
 
 def tile_cssrclassifier_pa_kernel(tc, d_bytes, d_scale, W_dec, x, out_0, out_1, out_2):
     nc = tc.nc
@@ -28,9 +26,13 @@ def tile_cssrclassifier_pa_kernel(tc, d_bytes, d_scale, W_dec, x, out_0, out_1, 
         work = ctx.enter_context(tc.tile_pool(name="work", bufs=2))
         psum = ctx.enter_context(tc.psum_pool(name="psum", bufs=2))
         ctx.enter_context(tc.manual_schedule())
+        BANKS = {"pp": 2, "qq": 3, "qs": 2, "tt": 1}
+
+        def bank(shape, dtype, name, tag):
+            return psum.tile(shape, dtype, name=name, tag=tag, bufs=BANKS[tag])
 
         sc = keep.tile([P, 4], F32, name="sc")
-        dbytes = [keep.tile([P, NIMG, 1024], U8, name="dbytes%d" % k) for k in range(NCLS)]
+        dbytes = [keep.tile([P, 4, NIMG, POS], U8, name="dbytes%d" % k) for k in range(NCLS)]
         wraw = [keep.tile([P, 4, HID], BF16, name="wraw%d" % k) for k in range(NCLS)]
         xraw = keep.tile([P, NIMG, 4, POS], BF16, name="xraw")
         xT = keep.tile([P, 8, CH], BF16, name="xT")
@@ -45,17 +47,11 @@ def tile_cssrclassifier_pa_kernel(tc, d_bytes, d_scale, W_dec, x, out_0, out_1, 
         x01 = keep.tile([P, 8], F32, name="x01")
         pmat = keep.tile([P, P], F32, name="pmat")
 
-        def load_d(k, b0, b1):
-            nc.sync.dma_start(
-                out=dbytes[k][:, b0:b1, :],
-                in_=d_bytes[k, b0:b1].rearrange("b (p t) y z -> p b (t y z)", t=4),
-            )
+        def load_d(k, b):
+            nc.sync.dma_start(out=dbytes[k][:, :, b, :], in_=d_bytes[k, b].rearrange("(p t) y z -> p t (y z)", t=4))
 
         def load_w(k):
-            nc.sync.dma_start(
-                out=wraw[k][:].rearrange("p i j -> p (i j)"),
-                in_=W_dec[k].rearrange("(m i) j -> m (i j)", i=4),
-            )
+            nc.sync.dma_start(out=wraw[k][:].rearrange("p i j -> p (i j)"), in_=W_dec[k].rearrange("(m i) j -> m (i j)", i=4))
 
         def load_x(b0, b1):
             nc.sync.dma_start(
@@ -64,16 +60,22 @@ def tile_cssrclassifier_pa_kernel(tc, d_bytes, d_scale, W_dec, x, out_0, out_1, 
             )
 
         nc.sync.dma_start(out=sc[:], in_=d_scale[0, 0, :, 0, 0].rearrange("(p t) -> p t", t=4))
-        load_d(0, 0, 2)
+        load_d(0, 0)
+        load_d(0, 1)
         load_w(0)
-        load_d(0, 2, 4)
+        load_d(0, 2)
+        load_d(0, 3)
         load_x(0, 2)
-        load_d(1, 0, 4)
+        for b in range(NIMG):
+            load_d(1, b)
         load_x(2, 4)
         load_w(1)
-        for k in range(2, NCLS):
-            load_d(k, 0, 4)
+        def load_class(k):
+            for b in range(NIMG):
+                load_d(k, b)
             load_w(k)
+
+        load_class(2)
 
         nc.gpsimd.memset(zer[:], 0.0)
         make_identity(nc, ident_f[:])
@@ -89,18 +91,15 @@ def tile_cssrclassifier_pa_kernel(tc, d_bytes, d_scale, W_dec, x, out_0, out_1, 
         wtp, wgrp, wq, wsc = {}, {}, {}, {}
         xtp, rst, ppt, qqt, qst = {}, {}, {}, {}, {}
 
-        def widen(s, lo, hi):
+        def widen(s, t, eng):
             k, h = divmod(s, 2)
-            if lo == 0:
+            if s not in wide:
                 wide[s] = work.tile([P, 4, 512], BF16, name="wide", tag="wide", bufs=3)
-            for idx in range(lo, hi):
-                b2, t = divmod(idx, 4)
-                nc.scalar.activation(
-                    out=wide[s][:, t, b2 * POS:(b2 + 1) * POS],
-                    in_=dbytes[k][:, 2 * h + b2, t * POS:(t + 1) * POS].bitcast(FP8),
-                    func=ACT.Copy,
-                    scale=sc[:, t:t + 1],
-                )
+            src = dbytes[k][:, t, 2 * h:2 * h + 2, :].rearrange("p b n -> p (b n)").bitcast(FP8)
+            if eng == "v":
+                nc.vector.tensor_scalar(out=wide[s][:, t, :], in0=src, scalar1=sc[:, t:t + 1], scalar2=None, op0=ALU.mult)
+            else:
+                nc.scalar.activation(out=wide[s][:, t, :], in_=src, func=ACT.Copy, scale=sc[:, t:t + 1])
 
         def interleave(s, b2, eng):
             if b2 == 0:
@@ -115,20 +114,15 @@ def tile_cssrclassifier_pa_kernel(tc, d_bytes, d_scale, W_dec, x, out_0, out_1, 
         def quant_d(s):
             dq[s] = work.tile([P, 512], U32, name="dq", tag="dq", bufs=3, align_bytes=64)
             dsc[s] = work.tile([P, 512], U8, name="dsc", tag="dsc", bufs=3, align_bytes=64)
-            nc.vector.quantize_mx(
-                out=dq[s][:].bitcast(FP8X4),
-                scales=dsc[s][:],
-                in_=grp[s][:].rearrange("p c t -> p (c t)"),
-            )
+            nc.vector.quantize_mx(out=dq[s][:].bitcast(FP8X4), scales=dsc[s][:], in_=grp[s][:].rearrange("p c t -> p (c t)"))
 
-        def wtrans(k):
-            for ii in range(2):
-                tp = psum.tile([P, 2, 2, P], F32, name="wtp", tag="tt")
-                wtp[(k, ii)] = tp
-                for i2 in range(2):
-                    words = wraw[k][:, 2 * ii + i2, :].bitcast(F32)
-                    for u in range(2):
-                        nc.tensor.transpose(tp[:, i2, u, :], words[:, u:256:2], ident_f[:])
+        def wtrans(k, ii, tag):
+            tp = bank([P, 2, 2, P], F32, "wtp", tag)
+            wtp[(k, ii)] = tp
+            for i2 in range(2):
+                words = wraw[k][:, 2 * ii + i2, :].bitcast(F32)
+                for u in range(2):
+                    nc.tensor.transpose(tp[:, i2, u, :], words[:, u:256:2], ident_f[:])
 
         def wevac(k, ii, eng):
             if ii == 0:
@@ -144,41 +138,36 @@ def tile_cssrclassifier_pa_kernel(tc, d_bytes, d_scale, W_dec, x, out_0, out_1, 
         def quant_w(k):
             wq[k] = work.tile([P, 512], U32, name="wq", tag="wq", bufs=2, align_bytes=64)
             wsc[k] = work.tile([P, 512], U8, name="wsc", tag="wsc", bufs=2, align_bytes=64)
-            nc.vector.quantize_mx(
-                out=wq[k][:].bitcast(FP8X4),
-                scales=wsc[k][:],
-                in_=wgrp[k][:].rearrange("p c t -> p (c t)"),
-            )
+            nc.vector.quantize_mx(out=wq[k][:].bitcast(FP8X4), scales=wsc[k][:], in_=wgrp[k][:].rearrange("p c t -> p (c t)"))
 
         def xtrans(u, tag):
             b, f = divmod(u, 2)
-            xp = psum.tile([P, 4, P], BF16, name="xtp", tag=tag)
+            xp = bank([P, 4, P], BF16, "xtp", tag)
             xtp[u] = xp
             for i in range(4):
                 nc.tensor.transpose(xp[:, i, :], xraw[:, b, i, f * P:(f + 1) * P], ident_b[:])
 
         def xevac(u):
-            nc.scalar.copy(out=xT[:, u, :], in_=xtp[u][:].rearrange("p i m -> p (i m)"))
+            nc.vector.tensor_copy(out=xT[:, u, :], in_=xtp[u][:].rearrange("p i m -> p (i m)"))
 
         def mm_p(s, i):
             k = s // 2
-            pp = psum.tile([P, 512], F32, name="pp", tag="pp")
+            pp = bank([P, 512], F32, "pp", "pp")
             ppt[(s, i)] = pp
             cols = slice(i * P, (i + 1) * P)
             nc.tensor.matmul_mx(
-                out=pp[:],
-                lhsT=wq[k][:, cols].bitcast(FP8X4), lhsT_scale=wsc[k][:, cols],
-                rhs=dq[s][:].bitcast(FP8X4), rhs_scale=dsc[s][:],
-                start=True, stop=True,
+                out=pp[:], lhsT=wq[k][:, cols].bitcast(FP8X4), lhsT_scale=wsc[k][:, cols],
+                rhs=dq[s][:].bitcast(FP8X4), rhs_scale=dsc[s][:], start=True, stop=True,
             )
 
         def rcopy(s, i, eng):
             if i == 0:
                 rst[s] = work.tile([P, 2, 4, POS], F32, name="rst", tag="rst", bufs=3)
+            src = ppt[(s, i)][:].rearrange("p (b n) -> p b n", b=2)
             if eng == "v":
-                nc.vector.tensor_copy(out=rst[s][:, :, i, :], in_=ppt[(s, i)][:].rearrange("p (b n) -> p b n", b=2))
+                nc.vector.tensor_copy(out=rst[s][:, :, i, :], in_=src)
             else:
-                nc.scalar.copy(out=rst[s][:, :, i, :], in_=ppt[(s, i)][:].rearrange("p (b n) -> p b n", b=2))
+                nc.scalar.copy(out=rst[s][:, :, i, :], in_=src)
 
         def store(s):
             k, h = divmod(s, 2)
@@ -187,30 +176,33 @@ def tile_cssrclassifier_pa_kernel(tc, d_bytes, d_scale, W_dec, x, out_0, out_1, 
                 in_=rst[s][:].rearrange("p b i n -> p b (i n)"),
             )
 
+        def store_part(s, i):
+            k, h = divmod(s, 2)
+            nc.sync.dma_start(
+                out=out_2[2 * h:2 * h + 2, k].rearrange("b (m i) y z -> i m b (y z)", i=4)[i],
+                in_=rst[s][:, :, i, :],
+            )
+
         def mm_q(s, v):
             k = s // 2
-            qq = psum.tile([P, 512], F32, name="qq", tag="qq")
+            qq = bank([P, 512], F32, "qq", "qq")
             qqt[(s, v)] = qq
             cols = slice(v * P, (v + 1) * P)
             nc.tensor.matmul_mx(
-                out=qq[:],
-                lhsT=dq[s][:, cols].bitcast(FP8X4), lhsT_scale=dsc[s][:, cols],
-                rhs=wq[k][:].bitcast(FP8X4), rhs_scale=wsc[k][:],
-                start=True, stop=True,
+                out=qq[:], lhsT=dq[s][:, cols].bitcast(FP8X4), lhsT_scale=dsc[s][:, cols],
+                rhs=wq[k][:].bitcast(FP8X4), rhs_scale=wsc[k][:], start=True, stop=True,
             )
 
         def mm_qs(s, v):
             k = s // 2
             if v == 0:
-                qst[s] = psum.tile([P, 4, P], F32, name="qs", tag="qs")
+                qst[s] = bank([P, 4, P], F32, "qs", "qs")
             cols = slice(v * P, (v + 1) * P)
             for i in range(4):
                 wc = slice(i * P, (i + 1) * P)
                 nc.tensor.matmul_mx(
-                    out=qst[s][:, v, :],
-                    lhsT=dq[s][:, cols].bitcast(FP8X4), lhsT_scale=dsc[s][:, cols],
-                    rhs=wq[k][:, wc].bitcast(FP8X4), rhs_scale=wsc[k][:, wc],
-                    start=(i == 0), stop=(i == 3),
+                    out=qst[s][:, v, :], lhsT=dq[s][:, cols].bitcast(FP8X4), lhsT_scale=dsc[s][:, cols],
+                    rhs=wq[k][:, wc].bitcast(FP8X4), rhs_scale=wsc[k][:, wc], start=(i == 0), stop=(i == 3),
                 )
 
         def stt(s, v):
@@ -224,89 +216,110 @@ def tile_cssrclassifier_pa_kernel(tc, d_bytes, d_scale, W_dec, x, out_0, out_1, 
         def red(s):
             nc.vector.tensor_reduce(out=asum[:, 4 * s:4 * s + 4], in_=qst[s][:], axis=AX.X, op=ALU.add)
 
-        widen(0, 0, 8)
-        wtrans(0)
+        widen(0, 0, "s")
+        widen(0, 1, "s")
+        widen(0, 2, "v")
+        widen(0, 3, "v")
+        wtrans(0, 0, "tt")
+        wtrans(0, 1, "pp")
         interleave(0, 0, "v")
-        wevac(0, 0, "v")
         interleave(0, 1, "v")
-        wevac(0, 1, "v")
-        quant_d(0)
+        wevac(0, 0, "s")
+        wevac(0, 1, "s")
+        widen(1, 0, "s")
+        widen(1, 1, "s")
+        widen(1, 2, "v")
+        widen(1, 3, "v")
         quant_w(0)
-        xtrans(0, "qq")
-        xtrans(1, "qq")
-        xtrans(2, "qs")
-        xtrans(3, "qs")
-        widen(1, 0, 4)
-        xevac(0)
-        xevac(1)
-        widen(1, 4, 8)
-        xevac(2)
-        xevac(3)
+        quant_d(0)
         interleave(1, 0, "g")
         interleave(1, 1, "g")
+        xtrans(0, "qq")
+        xtrans(1, "qq")
+        xtrans(2, "qq")
+        xtrans(3, "qs")
+        for u in range(4):
+            xevac(u)
+        widen(2, 0, "s")
+        widen(2, 1, "s")
 
         xs = None
-        for s in range(NSTEP):
+        LAST = NSTEP - 1
+        for s in range(LAST):
             k, h = divmod(s, 2)
             more_w = k + 1 < NCLS
+            if h == 0 and k + 3 < NCLS:
+                load_class(k + 3)
             for q in range(4):
                 mm_p(s, q)
                 mm_q(s, q)
                 mm_qs(s, q)
-                if s == 0 and q in (0, 2):
+                if q == 0 and s + 2 < NSTEP:
+                    widen(s + 2, 2, "s")
+                if q == 1:
+                    if s == 0:
+                        widen(2, 3, "s")
+                    elif more_w:
+                        wevac(k + 1, 0 if (s == 1 or h == 0) else 1, "s")
+                if q >= 2 and s + 3 < NSTEP:
+                    widen(s + 3, q - 2, "s")
+                if s == 1 and q == 2:
+                    wevac(1, 1, "s")
+                rcopy(s, q, "s")
+                if q == 3:
+                    store(s)
+                if s == 0:
                     xtrans(4 + q, "tt")
-                    xtrans(5 + q, "tt")
-                if more_w and ((k == 0 and h == 1 and q == 0) or (k > 0 and h == 0 and q == 2)):
-                    wtrans(k + 1)
-                if s == NSTEP - 2:
-                    if q == 0:
-                        xs = psum.tile([P, 8], F32, name="xs", tag="tt")
-                    for u in (2 * q, 2 * q + 1):
+                if s == 1 and q < 2:
+                    wtrans(1, q, "tt")
+                if s >= 2 and more_w and q == 0:
+                    wtrans(k + 1, h, "tt")
+                if (s == LAST - 2 and q >= 2) or (s == LAST - 1 and q < 2):
+                    if xs is None:
+                        xs = bank([P, 8], F32, "xs", "tt")
+                    j = q - 2 if s == LAST - 2 else q + 2
+                    for u in (2 * j, 2 * j + 1):
                         b, f = divmod(u, 2)
                         for i in range(4):
                             nc.tensor.matmul(
                                 out=xs[:, u:u + 1], lhsT=xraw[:, b, i, f * P:(f + 1) * P], rhs=ones_b[:, 0:1],
                                 start=(i == 0), stop=(i == 3),
                             )
-                if s + 2 < NSTEP:
-                    widen(s + 2, 2 * q, 2 * q + 2)
-                on_v = q in RC_ON_VECTOR and s + 2 < NSTEP
-                if not on_v:
-                    rcopy(s, q, "s")
-                if s == 0 and q in (1, 3):
-                    xevac(3 + q)
-                    xevac(4 + q)
-                if more_w and k == 0 and h == 1 and q in (1, 2):
-                    wevac(k + 1, q - 1, "s")
-                if more_w and k > 0 and h == 0 and q == 3:
-                    wevac(k + 1, 0, "s")
-                if more_w and k > 0 and h == 1 and q == 0:
-                    wevac(k + 1, 1, "s")
                 if q == 2:
-                    if more_w and k > 0 and h == 1:
+                    if s + 3 < NSTEP:
+                        widen(s + 3, 3, "v")
+                    if s >= 2 and more_w and h == 1:
                         quant_w(k + 1)
-                    if s + 1 < NSTEP:
-                        quant_d(s + 1)
-                if more_w and k == 0 and h == 1 and q == 3:
-                    quant_w(k + 1)
+                    quant_d(s + 1)
+                if s == 1 and q == 3:
+                    quant_w(1)
                 stt(s, q)
-                if on_v:
-                    rcopy(s, q, "v")
+                if s == 0:
+                    xevac(4 + q)
                 if q == 3:
                     red(s)
-                    if s == NSTEP - 2:
-                        nc.vector.tensor_scalar(out=x01[:], in0=xs[:], scalar1=0.1, scalar2=None, op0=ALU.mult)
-                    store(s)
-                if s + 2 < NSTEP and q >= 2:
-                    interleave(s + 2, q - 2, "g")
+                if q == 2 and s + 2 < NSTEP:
+                    interleave(s + 2, 0, "g")
+                    interleave(s + 2, 1, "g")
 
-        t1 = keep.tile([P, 64], F32, name="t1")
-        nc.vector.scalar_tensor_tensor(out=t1[:], in0=msum[:], scalar=2.0, in1=asum[:], op0=ALU.mult, op1=ALU.subtract)
-        lg0 = keep.tile([P, 64], F32, name="lg0")
+        for v in range(4):
+            mm_qs(LAST, v)
+        nc.vector.tensor_scalar(out=x01[:], in0=xs[:], scalar1=0.1, scalar2=None, op0=ALU.mult)
+        red(LAST)
+        axs = keep.tile([P, 64], F32, name="axs")
         nc.vector.scalar_tensor_tensor(
-            out=lg0[:].rearrange("p (k u) -> p k u", k=8), in0=t1[:].rearrange("p (k u) -> p k u", k=8), scalar=-0.1,
+            out=axs[:].rearrange("p (k u) -> p k u", k=8), in0=asum[:].rearrange("p (k u) -> p k u", k=8), scalar=0.1,
             in1=x01[:].rearrange("p (o u) -> p o u", o=1).to_broadcast([P, 8, 8]), op0=ALU.mult, op1=ALU.add,
         )
+        for q in range(4):
+            mm_q(LAST, q)
+            mm_p(LAST, q)
+            stt(LAST, q)
+            rcopy(LAST, q, "s")
+            store_part(LAST, q)
+
+        lg0 = keep.tile([P, 64], F32, name="lg0")
+        nc.vector.scalar_tensor_tensor(out=lg0[:], in0=msum[:], scalar=-0.2, in1=axs[:], op0=ALU.mult, op1=ALU.add)
         lg = keep.tile([P, 64], F32, name="lg")
         nc.vector.tensor_scalar(out=lg[:], in0=lg0[:], scalar1=-500.0, scalar2=500.0, op0=ALU.max, op1=ALU.min)
         mx = keep.tile([P, 8], F32, name="mx")
@@ -323,7 +336,7 @@ def tile_cssrclassifier_pa_kernel(tc, d_bytes, d_scale, W_dec, x, out_0, out_1, 
         nc.vector.tensor_tensor(
             out=lsum[:].rearrange("p (b k) -> p k b", b=4), in0=lg4[:, :, :, 0], in1=lg4[:, :, :, 1], op=ALU.add,
         )
-        er = psum.tile([P, 8], F32, name="er", tag="tt")
+        er = bank([P, 8], F32, "er", "qs")
         for b in range(NIMG):
             nc.tensor.matmul(out=er[:], lhsT=sel[:, b, :], rhs=lsum[:, b * 8:(b + 1) * 8], start=(b == 0), stop=(b == NIMG - 1))
         ers = keep.tile([P, 8], F32, name="ers")
@@ -338,7 +351,7 @@ def tile_cssrclassifier_pa_kernel(tc, d_bytes, d_scale, W_dec, x, out_0, out_1, 
             in0=ex[:].rearrange("p (k b f) -> p k b f", k=8, b=4),
             in1=rs[:].rearrange("p (o b f) -> p o b f", o=1, b=4).to_broadcast([P, 8, 4, 2]), op=ALU.mult,
         )
-        ptp = psum.tile([P, P], F32, name="ptp", tag="tt")
+        ptp = bank([P, P], F32, "ptp", "tt")
         nc.tensor.transpose(ptp[:], pmat[:], ident_f[:])
         pts = keep.tile([P, P], F32, name="pts")
         nc.vector.tensor_copy(out=pts[:], in_=ptp[:])

@@ -44,6 +44,7 @@ def tile_cssrclassifier_pa_kernel(tc, d_bytes, d_scale, W_dec, x, out_0, out_1, 
         sel = keep.tile([P, NIMG, P], F32, name="sel")
         msum = keep.tile([P, 64], F32, name="msum")
         asum = keep.tile([P, 64], F32, name="asum")
+        xsum = keep.tile([P, 8], F32, name="xsum")
         x01 = keep.tile([P, 8], F32, name="x01")
         pmat = keep.tile([P, P], F32, name="pmat")
 
@@ -243,68 +244,61 @@ def tile_cssrclassifier_pa_kernel(tc, d_bytes, d_scale, W_dec, x, out_0, out_1, 
         widen(2, 0, "s")
         widen(2, 1, "s")
 
-        xs = None
+        def xsum_part(u):
+            xjunk = work.tile([P, CH], BF16, name="xjunk", tag="xjunk", bufs=2)
+            nc.scalar.activation(out=xjunk[:], in_=xT[:, u, :], func=ACT.Copy, accum_out=xsum[:, u:u + 1])
+
         LAST = NSTEP - 1
         for s in range(LAST):
             k, h = divmod(s, 2)
             more_w = k + 1 < NCLS
+            qz = 2 if s == 0 else 1
             if h == 0 and k + 3 < NCLS:
                 load_class(k + 3)
             for q in range(4):
                 mm_p(s, q)
                 mm_q(s, q)
                 mm_qs(s, q)
-                if q == 0 and s + 2 < NSTEP:
+                if q == h and s + 2 < NSTEP:
                     widen(s + 2, 2, "s")
-                if q == 1:
-                    if s == 0:
-                        widen(2, 3, "s")
-                    elif more_w:
-                        wevac(k + 1, 0 if (s == 1 or h == 0) else 1, "s")
+                if s == 0 and q == 1:
+                    widen(2, 3, "s")
+                if more_w and ((s == 0 and q == 3) or (s >= 2 and h == 0 and q == 1)):
+                    wevac(k + 1, 0, "s")
+                if more_w and h == 1 and q == 0:
+                    wevac(k + 1, 1, "s")
                 if q >= 2 and s + 3 < NSTEP:
                     widen(s + 3, q - 2, "s")
-                if s == 1 and q == 2:
-                    wevac(1, 1, "s")
+                if s >= LAST - 2:
+                    xsum_part(4 * (s - LAST + 2) + q)
                 rcopy(s, q, "s")
                 if q == 3:
                     store(s)
-                if s == 0:
-                    xtrans(4 + q, "tt")
-                if s == 1 and q < 2:
-                    wtrans(1, q, "tt")
-                if s >= 2 and more_w and q == 0:
-                    wtrans(k + 1, h, "tt")
-                if (s == LAST - 2 and q >= 2) or (s == LAST - 1 and q < 2):
-                    if xs is None:
-                        xs = bank([P, 8], F32, "xs", "tt")
-                    j = q - 2 if s == LAST - 2 else q + 2
-                    for u in (2 * j, 2 * j + 1):
-                        b, f = divmod(u, 2)
-                        for i in range(4):
-                            nc.tensor.matmul(
-                                out=xs[:, u:u + 1], lhsT=xraw[:, b, i, f * P:(f + 1) * P], rhs=ones_b[:, 0:1],
-                                start=(i == 0), stop=(i == 3),
-                            )
-                if q == 2:
+                if 2 <= 4 * s + q < 6:
+                    xtrans(4 * s + q + 2, "qq")
+                if more_w and h == 0:
+                    if q == (2 if s == 0 else 0):
+                        wtrans(k + 1, 0, "tt")
+                    if q == (3 if s == 0 else 2):
+                        wtrans(k + 1, 1, "tt")
+                if q == qz:
                     if s + 3 < NSTEP:
                         widen(s + 3, 3, "v")
-                    if s >= 2 and more_w and h == 1:
+                    if more_w and h == 1:
                         quant_w(k + 1)
                     quant_d(s + 1)
-                if s == 1 and q == 3:
-                    quant_w(1)
                 stt(s, q)
-                if s == 0:
-                    xevac(4 + q)
+                if 2 <= 4 * s + q < 6:
+                    xevac(4 * s + q + 2)
                 if q == 3:
                     red(s)
-                if q == 2 and s + 2 < NSTEP:
+                if q == qz and s + 2 < NSTEP:
                     interleave(s + 2, 0, "g")
                     interleave(s + 2, 1, "g")
 
         for v in range(4):
             mm_qs(LAST, v)
-        nc.vector.tensor_scalar(out=x01[:], in0=xs[:], scalar1=0.1, scalar2=None, op0=ALU.mult)
+        nc.vector.tensor_scalar(out=x01[:], in0=xsum[:], scalar1=0.1, scalar2=None, op0=ALU.mult)
         red(LAST)
         axs = keep.tile([P, 64], F32, name="axs")
         nc.vector.scalar_tensor_tensor(

@@ -11,12 +11,21 @@ FP8 = mybir.dt.float8_e4m3fn
 FP8X4 = mybir.dt.float8_e4m3fn_x4
 ALU = mybir.AluOpType
 ACT = mybir.ActivationFunctionType
-AX = mybir.AxisListType
+AXIS = mybir.AxisListType
 
 NCLS, NIMG, CH, HID, POS = 8, 4, 512, 512, 256
 P = 128
-NSTEP = 2 * NCLS
+PACK = 4
+STEPS = 2 * NCLS
+LAST = STEPS - 1
+COLS = 2 * POS
+UNITS = 2 * NIMG
+REDUCTION = -0.1
+CLAMP = 500.0
 FLOPS = 2 * NCLS * NIMG * CH * HID * POS
+
+BANKS = {"recon": 2, "error": 3, "chsum": 2, "turn": 1}
+XSUM_STEPS = [3, 5, 7, 9]
 
 
 def tile_cssrclassifier_pa_kernel(tc, d_bytes, d_scale, W_dec, x, out_0, out_1, out_2):
@@ -26,30 +35,31 @@ def tile_cssrclassifier_pa_kernel(tc, d_bytes, d_scale, W_dec, x, out_0, out_1, 
         work = ctx.enter_context(tc.tile_pool(name="work", bufs=2))
         psum = ctx.enter_context(tc.psum_pool(name="psum", bufs=2))
         ctx.enter_context(tc.manual_schedule())
-        BANKS = {"pp": 2, "qq": 3, "qs": 2, "tt": 1}
 
         def bank(shape, dtype, name, tag):
             return psum.tile(shape, dtype, name=name, tag=tag, bufs=BANKS[tag])
 
-        sc = keep.tile([P, 4], F32, name="sc")
-        dbytes = [keep.tile([P, 4, NIMG, POS], U8, name="dbytes%d" % k) for k in range(NCLS)]
+        scale = keep.tile([P, PACK], F32, name="scale")
+        dbytes = [keep.tile([P, NIMG, PACK, POS], U8, name="dbytes%d" % k) for k in range(NCLS)]
         wraw = [keep.tile([P, 4, HID], BF16, name="wraw%d" % k) for k in range(NCLS)]
         xraw = keep.tile([P, NIMG, 4, POS], BF16, name="xraw")
-        xT = keep.tile([P, 8, CH], BF16, name="xT")
+        xT = keep.tile([P, UNITS, CH], BF16, name="xT")
         ident_f = keep.tile([P, P], F32, name="ident_f")
         ident_b = keep.tile([P, P], BF16, name="ident_b")
         ones_b = keep.tile([P, 2], BF16, name="ones_b")
-        zer = keep.tile([P, 1], F32, name="zer")
+        zero = keep.tile([P, 1], F32, name="zero")
         warm = keep.tile([P, 1], F32, name="warm")
-        sel = keep.tile([P, NIMG, P], F32, name="sel")
-        msum = keep.tile([P, 64], F32, name="msum")
-        asum = keep.tile([P, 64], F32, name="asum")
-        xsum = keep.tile([P, 8], F32, name="xsum")
-        x01 = keep.tile([P, 8], F32, name="x01")
+        pick = keep.tile([P, NIMG, P], F32, name="pick")
+        maxsum = keep.tile([P, NCLS * UNITS], F32, name="maxsum")
+        chsum = keep.tile([P, NCLS * UNITS], F32, name="chsum")
+        xsum01 = keep.tile([P, UNITS], F32, name="xsum01")
         pmat = keep.tile([P, P], F32, name="pmat")
 
-        def load_d(k, b):
-            nc.sync.dma_start(out=dbytes[k][:, :, b, :], in_=d_bytes[k, b].rearrange("(p t) y z -> p t (y z)", t=4))
+        def load_d(k, b0, b1):
+            nc.sync.dma_start(
+                out=dbytes[k][:, b0:b1].rearrange("p b t n -> p b (t n)"),
+                in_=d_bytes[k, b0:b1].rearrange("b (p t) y z -> p b (t y z)", t=PACK),
+            )
 
         def load_w(k):
             nc.sync.dma_start(out=wraw[k][:].rearrange("p i j -> p (i j)"), in_=W_dec[k].rearrange("(m i) j -> m (i j)", i=4))
@@ -60,293 +70,299 @@ def tile_cssrclassifier_pa_kernel(tc, d_bytes, d_scale, W_dec, x, out_0, out_1, 
                 in_=x[b0:b1].rearrange("b (m i) y z -> m b (i y z)", i=4),
             )
 
-        nc.sync.dma_start(out=sc[:], in_=d_scale[0, 0, :, 0, 0].rearrange("(p t) -> p t", t=4))
-        load_d(0, 0)
-        load_d(0, 1)
-        load_w(0)
-        load_d(0, 2)
-        load_d(0, 3)
-        load_x(0, 2)
-        for b in range(NIMG):
-            load_d(1, b)
-        load_x(2, 4)
-        load_w(1)
         def load_class(k):
-            for b in range(NIMG):
-                load_d(k, b)
+            load_d(k, 0, NIMG)
             load_w(k)
 
+        nc.sync.dma_start(out=scale[:], in_=d_scale[0, 0, :, 0, 0].rearrange("(p t) -> p t", t=PACK))
+        load_d(0, 0, 2)
+        load_w(0)
+        load_d(0, 2, 4)
+        load_x(0, 2)
+        load_d(1, 0, NIMG)
+        load_x(2, 4)
+        load_w(1)
         load_class(2)
 
-        nc.gpsimd.memset(zer[:], 0.0)
+        nc.gpsimd.memset(zero[:], 0.0)
         make_identity(nc, ident_f[:])
         make_identity(nc, ident_b[:])
         nc.gpsimd.memset(ones_b[:], 1.0)
-        nc.gpsimd.memset(sel[:], 0.0)
+        nc.gpsimd.memset(pick[:], 0.0)
         for b in range(NIMG):
-            nc.gpsimd.memset(sel[:, b, b:b + 1], 1.0 / POS)
+            nc.gpsimd.memset(pick[:, b, b:b + 1], 1.0 / POS)
         nc.gpsimd.memset(pmat[:], 0.0)
-        nc.scalar.activation(out=warm[:], in_=zer[:], func=ACT.Exp)
+        nc.scalar.activation(out=warm[:], in_=zero[:], func=ACT.Exp)
 
-        wide, grp, dq, dsc = {}, {}, {}, {}
-        wtp, wgrp, wq, wsc = {}, {}, {}, {}
-        xtp, rst, ppt, qqt, qst = {}, {}, {}, {}, {}
+        wide, grouped, dcodes, dscales = {}, {}, {}, {}
+        wturned, wgrouped, wcodes, wscales = {}, {}, {}, {}
+        xturned, xsum, staged, recon, error, chpart = {}, {}, {}, {}, {}, {}
 
-        def widen(s, t, eng):
+        def widen(s, t, engine):
             k, h = divmod(s, 2)
             if s not in wide:
-                wide[s] = work.tile([P, 4, 512], BF16, name="wide", tag="wide", bufs=3)
-            src = dbytes[k][:, t, 2 * h:2 * h + 2, :].rearrange("p b n -> p (b n)").bitcast(FP8)
-            if eng == "v":
-                nc.vector.tensor_scalar(out=wide[s][:, t, :], in0=src, scalar1=sc[:, t:t + 1], scalar2=None, op0=ALU.mult)
-            else:
-                nc.scalar.activation(out=wide[s][:, t, :], in_=src, func=ACT.Copy, scale=sc[:, t:t + 1])
+                wide[s] = work.tile([P, PACK, COLS], BF16, name="wide", tag="wide", bufs=3)
+            for b2 in range(2):
+                src = dbytes[k][:, 2 * h + b2, t, :].bitcast(FP8)
+                dst = wide[s][:, t, b2 * POS:(b2 + 1) * POS]
+                if engine == "vector":
+                    nc.vector.tensor_scalar(out=dst, in0=src, scalar1=scale[:, t:t + 1], scalar2=None, op0=ALU.mult)
+                else:
+                    nc.scalar.activation(out=dst, in_=src, func=ACT.Copy, scale=scale[:, t:t + 1])
 
-        def interleave(s, b2, eng):
+        def interleave(s, b2, engine):
             if b2 == 0:
-                grp[s] = work.tile([P, 512, 4], BF16, name="grp", tag="grp", bufs=1, align_bytes=64)
-            dst = grp[s][:, b2 * POS:(b2 + 1) * POS, :]
+                grouped[s] = work.tile([P, COLS, PACK], BF16, name="grouped", tag="grouped", bufs=1, align_bytes=64)
+            dst = grouped[s][:, b2 * POS:(b2 + 1) * POS, :]
             src = wide[s][:, :, b2 * POS:(b2 + 1) * POS].rearrange("p t c -> p c t")
-            if eng == "g":
+            if engine == "gpsimd":
                 nc.gpsimd.tensor_scalar(out=dst, in0=src, scalar1=1.0, scalar2=0.0, op0=ALU.mult, op1=ALU.add)
             else:
                 nc.vector.tensor_copy(out=dst, in_=src)
 
-        def quant_d(s):
-            dq[s] = work.tile([P, 512], U32, name="dq", tag="dq", bufs=3, align_bytes=64)
-            dsc[s] = work.tile([P, 512], U8, name="dsc", tag="dsc", bufs=3, align_bytes=64)
-            nc.vector.quantize_mx(out=dq[s][:].bitcast(FP8X4), scales=dsc[s][:], in_=grp[s][:].rearrange("p c t -> p (c t)"))
-
-        def wtrans(k, ii, tag):
-            tp = bank([P, 2, 2, P], F32, "wtp", tag)
-            wtp[(k, ii)] = tp
-            for i2 in range(2):
-                words = wraw[k][:, 2 * ii + i2, :].bitcast(F32)
-                for u in range(2):
-                    nc.tensor.transpose(tp[:, i2, u, :], words[:, u:256:2], ident_f[:])
-
-        def wevac(k, ii, eng):
-            if ii == 0:
-                wgrp[k] = work.tile([P, 512, 4], BF16, name="wgrp", tag="wgrp", bufs=2, align_bytes=64)
-            flat = wgrp[k][:].rearrange("p c t -> p (c t)").bitcast(F32)
-            dst = flat[:, ii * 512:(ii + 1) * 512].rearrange("p (i m u) -> p i m u", i=2, u=2)
-            src = wtp[(k, ii)][:].rearrange("p i u m -> p i m u")
-            if eng == "v":
-                nc.vector.tensor_copy(out=dst, in_=src)
-            else:
-                nc.scalar.copy(out=dst, in_=src)
-
-        def quant_w(k):
-            wq[k] = work.tile([P, 512], U32, name="wq", tag="wq", bufs=2, align_bytes=64)
-            wsc[k] = work.tile([P, 512], U8, name="wsc", tag="wsc", bufs=2, align_bytes=64)
-            nc.vector.quantize_mx(out=wq[k][:].bitcast(FP8X4), scales=wsc[k][:], in_=wgrp[k][:].rearrange("p c t -> p (c t)"))
-
-        def xtrans(u, tag):
-            b, f = divmod(u, 2)
-            xp = bank([P, 4, P], BF16, "xtp", tag)
-            xtp[u] = xp
-            for i in range(4):
-                nc.tensor.transpose(xp[:, i, :], xraw[:, b, i, f * P:(f + 1) * P], ident_b[:])
-
-        def xevac(u):
-            nc.vector.tensor_copy(out=xT[:, u, :], in_=xtp[u][:].rearrange("p i m -> p (i m)"))
-
-        def mm_p(s, i):
-            k = s // 2
-            pp = bank([P, 512], F32, "pp", "pp")
-            ppt[(s, i)] = pp
-            cols = slice(i * P, (i + 1) * P)
-            nc.tensor.matmul_mx(
-                out=pp[:], lhsT=wq[k][:, cols].bitcast(FP8X4), lhsT_scale=wsc[k][:, cols],
-                rhs=dq[s][:].bitcast(FP8X4), rhs_scale=dsc[s][:], start=True, stop=True,
+        def quantize_d(s):
+            dcodes[s] = work.tile([P, COLS], U32, name="dcodes", tag="dcodes", bufs=3, align_bytes=64)
+            dscales[s] = work.tile([P, COLS], U8, name="dscales", tag="dscales", bufs=3, align_bytes=64)
+            nc.vector.quantize_mx(
+                out=dcodes[s][:].bitcast(FP8X4), scales=dscales[s][:], in_=grouped[s][:].rearrange("p c t -> p (c t)"),
             )
 
-        def rcopy(s, i, eng):
-            if i == 0:
-                rst[s] = work.tile([P, 2, 4, POS], F32, name="rst", tag="rst", bufs=3)
-            src = ppt[(s, i)][:].rearrange("p (b n) -> p b n", b=2)
-            if eng == "v":
-                nc.vector.tensor_copy(out=rst[s][:, :, i, :], in_=src)
-            else:
-                nc.scalar.copy(out=rst[s][:, :, i, :], in_=src)
+        def turn_w(k, half, tag):
+            tp = bank([P, 2, 2, P], F32, "wturned", tag)
+            wturned[(k, half)] = tp
+            for i2 in range(2):
+                words = wraw[k][:, 2 * half + i2, :].bitcast(F32)
+                for u in range(2):
+                    nc.tensor.transpose(tp[:, i2, u, :], words[:, u:HID // 2:2], ident_f[:])
 
-        def store(s):
+        def group_w(k, half):
+            if half == 0:
+                wgrouped[k] = work.tile([P, CH, PACK], BF16, name="wgrouped", tag="wgrouped", bufs=2, align_bytes=64)
+            words = wgrouped[k][:].rearrange("p c t -> p (c t)").bitcast(F32)
+            nc.scalar.copy(
+                out=words[:, half * CH:(half + 1) * CH].rearrange("p (i m u) -> p i m u", i=2, u=2),
+                in_=wturned[(k, half)][:].rearrange("p i u m -> p i m u"),
+            )
+
+        def quantize_w(k):
+            wcodes[k] = work.tile([P, CH], U32, name="wcodes", tag="wcodes", bufs=2, align_bytes=64)
+            wscales[k] = work.tile([P, CH], U8, name="wscales", tag="wscales", bufs=2, align_bytes=64)
+            nc.vector.quantize_mx(
+                out=wcodes[k][:].bitcast(FP8X4), scales=wscales[k][:], in_=wgrouped[k][:].rearrange("p c t -> p (c t)"),
+            )
+
+        def turn_x(u, tag):
+            b, f = divmod(u, 2)
+            xturned[u] = bank([P, 4, P], BF16, "xturned", tag)
+            for i in range(4):
+                nc.tensor.transpose(xturned[u][:, i, :], xraw[:, b, i, f * P:(f + 1) * P], ident_b[:])
+
+        def keep_x(u):
+            nc.vector.tensor_copy(out=xT[:, u, :], in_=xturned[u][:].rearrange("p i m -> p (i m)"))
+
+        def sum_x(s):
+            xsum[s] = bank([P, 2], F32, "xsum", "turn")
+            for j in range(2):
+                b, f = divmod(2 * XSUM_STEPS.index(s) + j, 2)
+                for i in range(4):
+                    nc.tensor.matmul(
+                        out=xsum[s][:, j:j + 1], lhsT=xraw[:, b, i, f * P:(f + 1) * P], rhs=ones_b[:, 0:1],
+                        start=(i == 0), stop=(i == 3),
+                    )
+
+        def keep_xsum(s):
+            u0 = 2 * XSUM_STEPS.index(s)
+            nc.vector.tensor_scalar(out=xsum01[:, u0:u0 + 2], in0=xsum[s][:], scalar1=-REDUCTION, scalar2=None, op0=ALU.mult)
+
+        def mm_recon(s, i):
+            k = s // 2
+            recon[(s, i)] = bank([P, COLS], F32, "recon", "recon")
+            cols = slice(i * P, (i + 1) * P)
+            nc.tensor.matmul_mx(
+                out=recon[(s, i)][:], lhsT=wcodes[k][:, cols].bitcast(FP8X4), lhsT_scale=wscales[k][:, cols],
+                rhs=dcodes[s][:].bitcast(FP8X4), rhs_scale=dscales[s][:], start=True, stop=True,
+            )
+
+        def stage_recon(s, i):
+            if i == 0:
+                staged[s] = work.tile([P, 2, 4, POS], F32, name="staged", tag="staged", bufs=3)
+            nc.scalar.copy(out=staged[s][:, :, i, :], in_=recon[(s, i)][:].rearrange("p (b n) -> p b n", b=2))
+
+        def store_recon(s):
             k, h = divmod(s, 2)
             nc.sync.dma_start(
                 out=out_2[2 * h:2 * h + 2, k].rearrange("b (m i) y z -> m b (i y z)", i=4),
-                in_=rst[s][:].rearrange("p b i n -> p b (i n)"),
+                in_=staged[s][:].rearrange("p b i n -> p b (i n)"),
             )
 
-        def store_part(s, i):
+        def store_recon_part(s, i):
             k, h = divmod(s, 2)
             nc.sync.dma_start(
-                out=out_2[2 * h:2 * h + 2, k].rearrange("b (m i) y z -> i m b (y z)", i=4)[i],
-                in_=rst[s][:, :, i, :],
+                out=out_2[2 * h:2 * h + 2, k].rearrange("b (m i) y z -> i m b (y z)", i=4)[i], in_=staged[s][:, :, i, :],
             )
 
-        def mm_q(s, v):
+        def mm_error(s, v):
             k = s // 2
-            qq = bank([P, 512], F32, "qq", "qq")
-            qqt[(s, v)] = qq
+            error[(s, v)] = bank([P, CH], F32, "error", "error")
             cols = slice(v * P, (v + 1) * P)
             nc.tensor.matmul_mx(
-                out=qq[:], lhsT=dq[s][:, cols].bitcast(FP8X4), lhsT_scale=dsc[s][:, cols],
-                rhs=wq[k][:].bitcast(FP8X4), rhs_scale=wsc[k][:], start=True, stop=True,
+                out=error[(s, v)][:], lhsT=dcodes[s][:, cols].bitcast(FP8X4), lhsT_scale=dscales[s][:, cols],
+                rhs=wcodes[k][:].bitcast(FP8X4), rhs_scale=wscales[k][:], start=True, stop=True,
             )
 
-        def mm_qs(s, v):
+        def mm_chsum(s, v):
             k = s // 2
             if v == 0:
-                qst[s] = bank([P, 4, P], F32, "qs", "qs")
+                chpart[s] = bank([P, 4, P], F32, "chpart", "chsum")
             cols = slice(v * P, (v + 1) * P)
             for i in range(4):
-                wc = slice(i * P, (i + 1) * P)
+                group = slice(i * P, (i + 1) * P)
                 nc.tensor.matmul_mx(
-                    out=qst[s][:, v, :], lhsT=dq[s][:, cols].bitcast(FP8X4), lhsT_scale=dsc[s][:, cols],
-                    rhs=wq[k][:, wc].bitcast(FP8X4), rhs_scale=wsc[k][:, wc], start=(i == 0), stop=(i == 3),
+                    out=chpart[s][:, v, :], lhsT=dcodes[s][:, cols].bitcast(FP8X4), lhsT_scale=dscales[s][:, cols],
+                    rhs=wcodes[k][:, group].bitcast(FP8X4), rhs_scale=wscales[k][:, group], start=(i == 0), stop=(i == 3),
                 )
 
-        def stt(s, v):
-            h = s % 2
-            junk = work.tile([P, 512], F32, name="junk", tag="junk", bufs=2)
+        def sum_max(s, v):
+            unit = 4 * (s % 2) + v
+            maxima = work.tile([P, CH], F32, name="maxima", tag="maxima", bufs=2)
             nc.vector.scalar_tensor_tensor(
-                out=junk[:], in0=qqt[(s, v)][:], scalar=1.0, in1=xT[:, 4 * h + v, :],
-                op0=ALU.mult, op1=ALU.max, accum_out=msum[:, 4 * s + v:4 * s + v + 1],
+                out=maxima[:], in0=error[(s, v)][:], scalar=1.0, in1=xT[:, unit, :],
+                op0=ALU.mult, op1=ALU.max, accum_out=maxsum[:, 4 * s + v:4 * s + v + 1],
             )
 
-        def red(s):
-            nc.vector.tensor_reduce(out=asum[:, 4 * s:4 * s + 4], in_=qst[s][:], axis=AX.X, op=ALU.add)
+        def sum_channels(s):
+            nc.vector.tensor_reduce(out=chsum[:, 4 * s:4 * s + 4], in_=chpart[s][:], axis=AXIS.X, op=ALU.add)
 
-        widen(0, 0, "s")
-        widen(0, 1, "s")
-        widen(0, 2, "v")
-        widen(0, 3, "v")
-        wtrans(0, 0, "tt")
-        wtrans(0, 1, "pp")
-        interleave(0, 0, "v")
-        interleave(0, 1, "v")
-        wevac(0, 0, "s")
-        wevac(0, 1, "s")
-        widen(1, 0, "s")
-        widen(1, 1, "s")
-        widen(1, 2, "v")
-        widen(1, 3, "v")
-        quant_w(0)
-        quant_d(0)
-        interleave(1, 0, "g")
-        interleave(1, 1, "g")
-        xtrans(0, "qq")
-        xtrans(1, "qq")
-        xtrans(2, "qq")
-        xtrans(3, "qs")
+        widen(0, 0, "scalar")
+        widen(0, 1, "scalar")
+        widen(0, 2, "vector")
+        widen(0, 3, "vector")
+        turn_w(0, 0, "turn")
+        turn_w(0, 1, "recon")
+        interleave(0, 0, "vector")
+        interleave(0, 1, "vector")
+        group_w(0, 0)
+        group_w(0, 1)
+        widen(1, 0, "scalar")
+        widen(1, 1, "scalar")
+        widen(1, 2, "vector")
+        widen(1, 3, "vector")
+        quantize_w(0)
+        quantize_d(0)
+        interleave(1, 0, "gpsimd")
+        interleave(1, 1, "gpsimd")
+        turn_x(0, "error")
+        turn_x(1, "error")
+        turn_x(2, "error")
+        turn_x(3, "chsum")
         for u in range(4):
-            xevac(u)
-        widen(2, 0, "s")
-        widen(2, 1, "s")
+            keep_x(u)
+        widen(2, 0, "scalar")
+        widen(2, 1, "scalar")
 
-        def xsum_part(u):
-            xjunk = work.tile([P, CH], BF16, name="xjunk", tag="xjunk", bufs=2)
-            nc.scalar.activation(out=xjunk[:], in_=xT[:, u, :], func=ACT.Copy, accum_out=xsum[:, u:u + 1])
-
-        LAST = NSTEP - 1
         for s in range(LAST):
             k, h = divmod(s, 2)
             more_w = k + 1 < NCLS
-            qz = 2 if s == 0 else 1
+            quant = 2 if s == 0 else 1
+            turn_after = (2, 3) if s == 0 else (0, 2)
             if h == 0 and k + 3 < NCLS:
                 load_class(k + 3)
             for q in range(4):
-                mm_p(s, q)
-                mm_q(s, q)
-                mm_qs(s, q)
-                if q == h and s + 2 < NSTEP:
-                    widen(s + 2, 2, "s")
+                mm_recon(s, q)
+                mm_error(s, q)
+                mm_chsum(s, q)
+                if q == h and s + 2 < STEPS:
+                    widen(s + 2, 2, "scalar")
                 if s == 0 and q == 1:
-                    widen(2, 3, "s")
-                if more_w and ((s == 0 and q == 3) or (s >= 2 and h == 0 and q == 1)):
-                    wevac(k + 1, 0, "s")
+                    widen(2, 3, "scalar")
+                if more_w and h == 0 and q == turn_after[0] + 1:
+                    group_w(k + 1, 0)
                 if more_w and h == 1 and q == 0:
-                    wevac(k + 1, 1, "s")
-                if q >= 2 and s + 3 < NSTEP:
-                    widen(s + 3, q - 2, "s")
-                if s >= LAST - 2:
-                    xsum_part(4 * (s - LAST + 2) + q)
-                rcopy(s, q, "s")
+                    group_w(k + 1, 1)
+                if q >= 2 and s + 3 < STEPS:
+                    widen(s + 3, q - 2, "scalar")
+                stage_recon(s, q)
                 if q == 3:
-                    store(s)
+                    store_recon(s)
                 if 2 <= 4 * s + q < 6:
-                    xtrans(4 * s + q + 2, "qq")
-                if more_w and h == 0:
-                    if q == (2 if s == 0 else 0):
-                        wtrans(k + 1, 0, "tt")
-                    if q == (3 if s == 0 else 2):
-                        wtrans(k + 1, 1, "tt")
-                if q == qz:
-                    if s + 3 < NSTEP:
-                        widen(s + 3, 3, "v")
+                    turn_x(4 * s + q + 2, "error")
+                if s in XSUM_STEPS and q == 1:
+                    sum_x(s)
+                if more_w and h == 0 and q in turn_after:
+                    turn_w(k + 1, turn_after.index(q), "turn")
+                if q == quant:
+                    if s + 3 < STEPS:
+                        widen(s + 3, 3, "vector")
                     if more_w and h == 1:
-                        quant_w(k + 1)
-                    quant_d(s + 1)
-                stt(s, q)
+                        quantize_w(k + 1)
+                    quantize_d(s + 1)
+                sum_max(s, q)
+                if s in XSUM_STEPS and q == 2:
+                    keep_xsum(s)
                 if 2 <= 4 * s + q < 6:
-                    xevac(4 * s + q + 2)
+                    keep_x(4 * s + q + 2)
                 if q == 3:
-                    red(s)
-                if q == qz and s + 2 < NSTEP:
-                    interleave(s + 2, 0, "g")
-                    interleave(s + 2, 1, "g")
+                    sum_channels(s)
+                if q == quant and s + 2 < STEPS:
+                    interleave(s + 2, 0, "gpsimd")
+                    interleave(s + 2, 1, "gpsimd")
 
         for v in range(4):
-            mm_qs(LAST, v)
-        nc.vector.tensor_scalar(out=x01[:], in0=xsum[:], scalar1=0.1, scalar2=None, op0=ALU.mult)
-        red(LAST)
-        axs = keep.tile([P, 64], F32, name="axs")
+            mm_chsum(LAST, v)
+        sum_channels(LAST)
+        by_class = "p (k u) -> p k u"
+        over_classes = "p (k u) -> p u k"
+        linear = keep.tile([P, NCLS * UNITS], F32, name="linear")
         nc.vector.scalar_tensor_tensor(
-            out=axs[:].rearrange("p (k u) -> p k u", k=8), in0=asum[:].rearrange("p (k u) -> p k u", k=8), scalar=0.1,
-            in1=x01[:].rearrange("p (o u) -> p o u", o=1).to_broadcast([P, 8, 8]), op0=ALU.mult, op1=ALU.add,
+            out=linear[:].rearrange(by_class, k=NCLS), in0=chsum[:].rearrange(by_class, k=NCLS), scalar=-REDUCTION,
+            in1=xsum01[:].rearrange("p (o u) -> p o u", o=1).to_broadcast([P, NCLS, UNITS]), op0=ALU.mult, op1=ALU.add,
         )
         for q in range(4):
-            mm_q(LAST, q)
-            mm_p(LAST, q)
-            stt(LAST, q)
-            rcopy(LAST, q, "s")
-            store_part(LAST, q)
+            mm_error(LAST, q)
+            mm_recon(LAST, q)
+            sum_max(LAST, q)
+            stage_recon(LAST, q)
+            store_recon_part(LAST, q)
 
-        lg0 = keep.tile([P, 64], F32, name="lg0")
-        nc.vector.scalar_tensor_tensor(out=lg0[:], in0=msum[:], scalar=-0.2, in1=axs[:], op0=ALU.mult, op1=ALU.add)
-        lg = keep.tile([P, 64], F32, name="lg")
-        nc.vector.tensor_scalar(out=lg[:], in0=lg0[:], scalar1=-500.0, scalar2=500.0, op0=ALU.max, op1=ALU.min)
-        mx = keep.tile([P, 8], F32, name="mx")
-        nc.vector.tensor_reduce(out=mx[:], in_=lg[:].rearrange("p (k u) -> p u k", k=8), axis=AX.X, op=ALU.max)
-        sh = keep.tile([P, 64], F32, name="sh")
+        raw = keep.tile([P, NCLS * UNITS], F32, name="raw")
+        nc.vector.scalar_tensor_tensor(out=raw[:], in0=maxsum[:], scalar=2.0 * REDUCTION, in1=linear[:], op0=ALU.mult, op1=ALU.add)
+        logits = keep.tile([P, NCLS * UNITS], F32, name="logits")
+        nc.vector.tensor_scalar(out=logits[:], in0=raw[:], scalar1=-CLAMP, scalar2=CLAMP, op0=ALU.max, op1=ALU.min)
+        top = keep.tile([P, UNITS], F32, name="top")
+        nc.vector.tensor_reduce(out=top[:], in_=logits[:].rearrange(over_classes, k=NCLS), axis=AXIS.X, op=ALU.max)
+        shifted = keep.tile([P, NCLS * UNITS], F32, name="shifted")
         nc.vector.tensor_tensor(
-            out=sh[:].rearrange("p (k u) -> p k u", k=8), in0=lg[:].rearrange("p (k u) -> p k u", k=8),
-            in1=mx[:].rearrange("p (o u) -> p o u", o=1).to_broadcast([P, 8, 8]), op=ALU.subtract,
+            out=shifted[:].rearrange(by_class, k=NCLS), in0=logits[:].rearrange(by_class, k=NCLS),
+            in1=top[:].rearrange("p (o u) -> p o u", o=1).to_broadcast([P, NCLS, UNITS]), op=ALU.subtract,
         )
-        ex = keep.tile([P, 64], F32, name="ex")
-        nc.scalar.activation(out=ex[:], in_=sh[:], func=ACT.Exp)
-        lsum = keep.tile([P, 32], F32, name="lsum")
-        lg4 = lg[:].rearrange("p (k b f) -> p k b f", k=8, b=4)
+        expd = keep.tile([P, NCLS * UNITS], F32, name="expd")
+        nc.scalar.activation(out=expd[:], in_=shifted[:], func=ACT.Exp)
+
+        halves = keep.tile([P, NIMG * NCLS], F32, name="halves")
+        split = logits[:].rearrange("p (k b f) -> p k b f", k=NCLS, b=NIMG)
         nc.vector.tensor_tensor(
-            out=lsum[:].rearrange("p (b k) -> p k b", b=4), in0=lg4[:, :, :, 0], in1=lg4[:, :, :, 1], op=ALU.add,
+            out=halves[:].rearrange("p (b k) -> p k b", b=NIMG), in0=split[:, :, :, 0], in1=split[:, :, :, 1], op=ALU.add,
         )
-        er = bank([P, 8], F32, "er", "qs")
+        pooled = bank([P, NCLS], F32, "pooled", "chsum")
         for b in range(NIMG):
-            nc.tensor.matmul(out=er[:], lhsT=sel[:, b, :], rhs=lsum[:, b * 8:(b + 1) * 8], start=(b == 0), stop=(b == NIMG - 1))
-        ers = keep.tile([P, 8], F32, name="ers")
-        nc.scalar.copy(out=ers[:], in_=er[:])
-        nc.sync.dma_start(out=out_1, in_=ers[0:4, :])
-        sm = keep.tile([P, 8], F32, name="sm")
-        nc.vector.tensor_reduce(out=sm[:], in_=ex[:].rearrange("p (k u) -> p u k", k=8), axis=AX.X, op=ALU.add)
-        rs = keep.tile([P, 8], F32, name="rs")
-        nc.vector.reciprocal(out=rs[:], in_=sm[:])
+            nc.tensor.matmul(
+                out=pooled[:], lhsT=pick[:, b, :], rhs=halves[:, b * NCLS:(b + 1) * NCLS], start=(b == 0), stop=(b == NIMG - 1),
+            )
+        pooled_sb = keep.tile([P, NCLS], F32, name="pooled_sb")
+        nc.scalar.copy(out=pooled_sb[:], in_=pooled[:])
+        nc.sync.dma_start(out=out_1, in_=pooled_sb[0:NIMG, :])
+
+        total = keep.tile([P, UNITS], F32, name="total")
+        nc.vector.tensor_reduce(out=total[:], in_=expd[:].rearrange(over_classes, k=NCLS), axis=AXIS.X, op=ALU.add)
+        inverse = keep.tile([P, UNITS], F32, name="inverse")
+        nc.vector.reciprocal(out=inverse[:], in_=total[:])
         nc.vector.tensor_tensor(
-            out=pmat[:, 0:64].rearrange("p (b k f) -> p k b f", b=4, k=8),
-            in0=ex[:].rearrange("p (k b f) -> p k b f", k=8, b=4),
-            in1=rs[:].rearrange("p (o b f) -> p o b f", o=1, b=4).to_broadcast([P, 8, 4, 2]), op=ALU.mult,
+            out=pmat[:, 0:NCLS * UNITS].rearrange("p (b k f) -> p k b f", b=NIMG, k=NCLS),
+            in0=expd[:].rearrange("p (k b f) -> p k b f", k=NCLS, b=NIMG),
+            in1=inverse[:].rearrange("p (o b f) -> p o b f", o=1, b=NIMG).to_broadcast([P, NCLS, NIMG, 2]), op=ALU.mult,
         )
-        ptp = bank([P, P], F32, "ptp", "tt")
-        nc.tensor.transpose(ptp[:], pmat[:], ident_f[:])
-        pts = keep.tile([P, P], F32, name="pts")
-        nc.vector.tensor_copy(out=pts[:], in_=ptp[:])
-        nc.sync.dma_start(out=out_0.rearrange("b k (f g) w -> (b k f) (g w)", f=2), in_=pts[0:64, :])
+        pturned = bank([P, P], F32, "pturned", "turn")
+        nc.tensor.transpose(pturned[:], pmat[:], ident_f[:])
+        prows = keep.tile([P, P], F32, name="prows")
+        nc.vector.tensor_copy(out=prows[:], in_=pturned[:])
+        nc.sync.dma_start(out=out_0.rearrange("b k (f g) w -> (b k f) (g w)", f=2), in_=prows[0:NCLS * UNITS, :])

@@ -26,6 +26,8 @@ FLOPS = 2 * NCLS * NIMG * CH * HID * POS
 
 BANKS = {"recon": 2, "error": 3, "chsum": 2, "turn": 1}
 XSUM_STEPS = [3, 5, 7, 9]
+SPIN_FIRST = 7
+SPIN_BETWEEN = 2
 
 
 def tile_cssrclassifier_pa_kernel(tc, d_bytes, d_scale, W_dec, x, out_0, out_1, out_2):
@@ -54,6 +56,7 @@ def tile_cssrclassifier_pa_kernel(tc, d_bytes, d_scale, W_dec, x, out_0, out_1, 
         chsum = keep.tile([P, NCLS * UNITS], F32, name="chsum")
         xsum01 = keep.tile([P, UNITS], F32, name="xsum01")
         pmat = keep.tile([P, P], F32, name="pmat")
+        nothing = keep.tile([P, COLS], BF16, name="nothing")
 
         def load_d(k, b0, b1):
             nc.sync.dma_start(
@@ -84,6 +87,7 @@ def tile_cssrclassifier_pa_kernel(tc, d_bytes, d_scale, W_dec, x, out_0, out_1, 
         load_w(1)
         load_class(2)
 
+        nc.vector.memset(nothing[:], 0.0)
         nc.gpsimd.memset(zero[:], 0.0)
         make_identity(nc, ident_f[:])
         make_identity(nc, ident_b[:])
@@ -233,12 +237,20 @@ def tile_cssrclassifier_pa_kernel(tc, d_bytes, d_scale, W_dec, x, out_0, out_1, 
         def sum_channels(s):
             nc.vector.tensor_reduce(out=chsum[:, 4 * s:4 * s + 4], in_=chpart[s][:], axis=AXIS.X, op=ALU.add)
 
+        unread = bank([P, COLS], F32, "unread", "chsum")
+
+        def spin(count):
+            for n in range(count):
+                nc.tensor.matmul(out=unread[:], lhsT=nothing[:, 0:P], rhs=nothing[:], start=True, stop=True)
+
+        spin(SPIN_FIRST)
         widen(0, 0, "scalar")
         widen(0, 1, "scalar")
         widen(0, 2, "vector")
         widen(0, 3, "vector")
         turn_w(0, 0, "turn")
         turn_w(0, 1, "recon")
+        spin(SPIN_BETWEEN)
         interleave(0, 0, "vector")
         interleave(0, 1, "vector")
         group_w(0, 0)
@@ -255,6 +267,7 @@ def tile_cssrclassifier_pa_kernel(tc, d_bytes, d_scale, W_dec, x, out_0, out_1, 
         turn_x(1, "error")
         turn_x(2, "error")
         turn_x(3, "chsum")
+        spin(SPIN_BETWEEN)
         for u in range(4):
             keep_x(u)
         widen(2, 0, "scalar")

@@ -28,6 +28,8 @@ BANKS = {"recon": 2, "error": 3, "chsum": 2, "turn": 1}
 XSUM_STEPS = [3, 5, 7, 9]
 SPIN_FIRST = 7
 SPIN_BETWEEN = 2
+SCALAR_SUM_STEPS = [13, 14]
+SCALAR_UNITS = 2
 
 
 def tile_cssrclassifier_pa_kernel(tc, d_bytes, d_scale, W_dec, x, out_0, out_1, out_2):
@@ -234,8 +236,16 @@ def tile_cssrclassifier_pa_kernel(tc, d_bytes, d_scale, W_dec, x, out_0, out_1, 
                 op0=ALU.mult, op1=ALU.max, accum_out=maxsum[:, 4 * s + v:4 * s + v + 1],
             )
 
+        def units_on_tensor(s):
+            return 4 - SCALAR_UNITS if s in SCALAR_SUM_STEPS else 4
+
         def sum_channels(s):
-            nc.vector.tensor_reduce(out=chsum[:, 4 * s:4 * s + 4], in_=chpart[s][:], axis=AXIS.X, op=ALU.add)
+            n = units_on_tensor(s)
+            nc.vector.tensor_reduce(out=chsum[:, 4 * s:4 * s + n], in_=chpart[s][:, 0:n, :], axis=AXIS.X, op=ALU.add)
+
+        def sum_channels_scalar(s, v):
+            copied = work.tile([P, CH], F32, name="copied", tag="copied", bufs=2)
+            nc.scalar.activation(out=copied[:], in_=error[(s, v)][:], func=ACT.Copy, accum_out=chsum[:, 4 * s + v:4 * s + v + 1])
 
         unread = bank([P, COLS], F32, "unread", "chsum")
 
@@ -283,7 +293,8 @@ def tile_cssrclassifier_pa_kernel(tc, d_bytes, d_scale, W_dec, x, out_0, out_1, 
             for q in range(4):
                 mm_recon(s, q)
                 mm_error(s, q)
-                mm_chsum(s, q)
+                if q < units_on_tensor(s):
+                    mm_chsum(s, q)
                 if q == h and s + 2 < STEPS:
                     widen(s + 2, 2, "scalar")
                 if s == 0 and q == 1:
@@ -295,6 +306,8 @@ def tile_cssrclassifier_pa_kernel(tc, d_bytes, d_scale, W_dec, x, out_0, out_1, 
                 if q >= 2 and s + 3 < STEPS:
                     widen(s + 3, q - 2, "scalar")
                 stage_recon(s, q)
+                if q >= units_on_tensor(s):
+                    sum_channels_scalar(s, q)
                 if q == 3:
                     store_recon(s)
                 if 2 <= 4 * s + q < 6:
@@ -314,7 +327,7 @@ def tile_cssrclassifier_pa_kernel(tc, d_bytes, d_scale, W_dec, x, out_0, out_1, 
                     keep_xsum(s)
                 if 2 <= 4 * s + q < 6:
                     keep_x(4 * s + q + 2)
-                if q == 3:
+                if q == units_on_tensor(s) - 1:
                     sum_channels(s)
                 if q == quant and s + 2 < STEPS:
                     interleave(s + 2, 0, "gpsimd")
@@ -341,6 +354,11 @@ def tile_cssrclassifier_pa_kernel(tc, d_bytes, d_scale, W_dec, x, out_0, out_1, 
         nc.vector.scalar_tensor_tensor(out=raw[:], in0=maxsum[:], scalar=2.0 * REDUCTION, in1=linear[:], op0=ALU.mult, op1=ALU.add)
         logits = keep.tile([P, NCLS * UNITS], F32, name="logits")
         nc.vector.tensor_scalar(out=logits[:], in0=raw[:], scalar1=-CLAMP, scalar2=CLAMP, op0=ALU.max, op1=ALU.min)
+        halves = keep.tile([P, NIMG * NCLS], F32, name="halves")
+        split = logits[:].rearrange("p (k b f) -> p k b f", k=NCLS, b=NIMG)
+        nc.vector.tensor_tensor(
+            out=halves[:].rearrange("p (b k) -> p k b", b=NIMG), in0=split[:, :, :, 0], in1=split[:, :, :, 1], op=ALU.add,
+        )
         top = keep.tile([P, UNITS], F32, name="top")
         nc.vector.tensor_reduce(out=top[:], in_=logits[:].rearrange(over_classes, k=NCLS), axis=AXIS.X, op=ALU.max)
         shifted = keep.tile([P, NCLS * UNITS], F32, name="shifted")
@@ -351,11 +369,6 @@ def tile_cssrclassifier_pa_kernel(tc, d_bytes, d_scale, W_dec, x, out_0, out_1, 
         expd = keep.tile([P, NCLS * UNITS], F32, name="expd")
         nc.scalar.activation(out=expd[:], in_=shifted[:], func=ACT.Exp)
 
-        halves = keep.tile([P, NIMG * NCLS], F32, name="halves")
-        split = logits[:].rearrange("p (k b f) -> p k b f", k=NCLS, b=NIMG)
-        nc.vector.tensor_tensor(
-            out=halves[:].rearrange("p (b k) -> p k b", b=NIMG), in0=split[:, :, :, 0], in1=split[:, :, :, 1], op=ALU.add,
-        )
         pooled = bank([P, NCLS], F32, "pooled", "chsum")
         for b in range(NIMG):
             nc.tensor.matmul(

@@ -24,7 +24,7 @@ REDUCTION = -0.1
 CLAMP = 500.0
 FLOPS = 2 * NCLS * NIMG * CH * HID * POS
 
-BANKS = {"recon": 2, "error": 3, "chsum": 2, "turn": 1}
+BANKS = {"recon": 2, "error": 4, "chsum": 2}
 XSUM_STEPS = [3, 5, 7, 9]
 SPIN_FIRST = 7
 SPIN_BETWEEN = 2
@@ -167,7 +167,7 @@ def tile_cssrclassifier_pa_kernel(tc, d_bytes, d_scale, W_dec, x, out_0, out_1, 
             nc.vector.tensor_copy(out=xT[:, u, :], in_=xturned[u][:].rearrange("p i m -> p (i m)"))
 
         def sum_x(s):
-            xsum[s] = bank([P, 2], F32, "xsum", "turn")
+            xsum[s] = bank([P, 2], F32, "xsum", "error")
             for j in range(2):
                 b, f = divmod(2 * XSUM_STEPS.index(s) + j, 2)
                 for i in range(4):
@@ -258,7 +258,7 @@ def tile_cssrclassifier_pa_kernel(tc, d_bytes, d_scale, W_dec, x, out_0, out_1, 
         widen(0, 1, "scalar")
         widen(0, 2, "vector")
         widen(0, 3, "vector")
-        turn_w(0, 0, "turn")
+        turn_w(0, 0, "error")
         turn_w(0, 1, "recon")
         spin(SPIN_BETWEEN)
         interleave(0, 0, "vector")
@@ -315,7 +315,7 @@ def tile_cssrclassifier_pa_kernel(tc, d_bytes, d_scale, W_dec, x, out_0, out_1, 
                 if s in XSUM_STEPS and q == 1:
                     sum_x(s)
                 if more_w and h == 0 and q in turn_after:
-                    turn_w(k + 1, turn_after.index(q), "turn")
+                    turn_w(k + 1, turn_after.index(q), "error")
                 if q == quant:
                     if s + 3 < STEPS:
                         widen(s + 3, 3, "vector")
@@ -387,7 +387,7 @@ def tile_cssrclassifier_pa_kernel(tc, d_bytes, d_scale, W_dec, x, out_0, out_1, 
             in0=expd[:].rearrange("p (k b f) -> p k b f", k=NCLS, b=NIMG),
             in1=inverse[:].rearrange("p (o b f) -> p o b f", o=1, b=NIMG).to_broadcast([P, NCLS, NIMG, 2]), op=ALU.mult,
         )
-        pturned = bank([P, P], F32, "pturned", "turn")
+        pturned = bank([P, P], F32, "pturned", "recon")
         nc.tensor.transpose(pturned[:], pmat[:], ident_f[:])
         prows = keep.tile([P, P], F32, name="prows")
         nc.vector.tensor_copy(out=prows[:], in_=pturned[:])

@@ -335,7 +335,9 @@ def tile_cssrclassifier_pa_kernel(tc, d_bytes, d_scale, W_dec, x, out_0, out_1, 
 
         for v in range(4):
             mm_chsum(LAST, v)
-        sum_channels(LAST)
+        for v in range(4):
+            part = work.tile([P, P], BF16, name="part", tag="part", bufs=2)
+            nc.scalar.activation(out=part[:], in_=chpart[LAST][:, v, :], func=ACT.Copy, accum_out=chsum[:, 4 * LAST + v:4 * LAST + v + 1])
         by_class = "p (k u) -> p k u"
         over_classes = "p (k u) -> p u k"
         linear = keep.tile([P, NCLS * UNITS], F32, name="linear")

@@ -25,7 +25,6 @@ CLAMP = 500.0
 FLOPS = 2 * NCLS * NIMG * CH * HID * POS
 
 BANKS = {"recon": 2, "error": 4, "chsum": 2}
-XSUM_STEPS = [3, 5, 7, 9]
 SPIN_FIRST = 7
 SPIN_BETWEEN = 2
 SCALAR_SUM_STEPS = [13, 14]
@@ -50,12 +49,12 @@ def tile_cssrclassifier_pa_kernel(tc, d_bytes, d_scale, W_dec, x, out_0, out_1, 
         xT = keep.tile([P, UNITS, CH], BF16, name="xT")
         ident_f = keep.tile([P, P], F32, name="ident_f")
         ident_b = keep.tile([P, P], BF16, name="ident_b")
-        ones_b = keep.tile([P, 2], BF16, name="ones_b")
         zero = keep.tile([P, 1], F32, name="zero")
         warm = keep.tile([P, 1], F32, name="warm")
         pick = keep.tile([P, NIMG, P], F32, name="pick")
         maxsum = keep.tile([P, NCLS * UNITS], F32, name="maxsum")
         chsum = keep.tile([P, NCLS * UNITS], F32, name="chsum")
+        xsum = keep.tile([P, UNITS], F32, name="xsum")
         xsum01 = keep.tile([P, UNITS], F32, name="xsum01")
         pmat = keep.tile([P, P], F32, name="pmat")
         nothing = keep.tile([P, COLS], BF16, name="nothing")
@@ -93,7 +92,6 @@ def tile_cssrclassifier_pa_kernel(tc, d_bytes, d_scale, W_dec, x, out_0, out_1, 
         nc.gpsimd.memset(zero[:], 0.0)
         make_identity(nc, ident_f[:])
         make_identity(nc, ident_b[:])
-        nc.gpsimd.memset(ones_b[:], 1.0)
         nc.gpsimd.memset(pick[:], 0.0)
         for b in range(NIMG):
             nc.gpsimd.memset(pick[:, b, b:b + 1], 1.0 / POS)
@@ -102,7 +100,7 @@ def tile_cssrclassifier_pa_kernel(tc, d_bytes, d_scale, W_dec, x, out_0, out_1, 
 
         wide, grouped, dcodes, dscales = {}, {}, {}, {}
         wturned, wgrouped, wcodes, wscales = {}, {}, {}, {}
-        xturned, xsum, staged, recon, error, chpart = {}, {}, {}, {}, {}, {}
+        xturned, staged, recon, error, chpart = {}, {}, {}, {}, {}
 
         def widen(s, t, engine):
             k, h = divmod(s, 2)
@@ -164,21 +162,10 @@ def tile_cssrclassifier_pa_kernel(tc, d_bytes, d_scale, W_dec, x, out_0, out_1, 
                 nc.tensor.transpose(xturned[u][:, i, :], xraw[:, b, i, f * P:(f + 1) * P], ident_b[:])
 
         def keep_x(u):
-            nc.vector.tensor_copy(out=xT[:, u, :], in_=xturned[u][:].rearrange("p i m -> p (i m)"))
-
-        def sum_x(s):
-            xsum[s] = bank([P, 2], F32, "xsum", "error")
-            for j in range(2):
-                b, f = divmod(2 * XSUM_STEPS.index(s) + j, 2)
-                for i in range(4):
-                    nc.tensor.matmul(
-                        out=xsum[s][:, j:j + 1], lhsT=xraw[:, b, i, f * P:(f + 1) * P], rhs=ones_b[:, 0:1],
-                        start=(i == 0), stop=(i == 3),
-                    )
-
-        def keep_xsum(s):
-            u0 = 2 * XSUM_STEPS.index(s)
-            nc.vector.tensor_scalar(out=xsum01[:, u0:u0 + 2], in0=xsum[s][:], scalar1=-REDUCTION, scalar2=None, op0=ALU.mult)
+            nc.vector.tensor_scalar(
+                out=xT[:, u, :], in0=xturned[u][:].rearrange("p i m -> p (i m)"), scalar1=1.0, scalar2=None,
+                op0=ALU.mult, op1=ALU.add, accum_out=xsum[:, u:u + 1],
+            )
 
         def mm_recon(s, i):
             k = s // 2
@@ -312,8 +299,6 @@ def tile_cssrclassifier_pa_kernel(tc, d_bytes, d_scale, W_dec, x, out_0, out_1, 
                     store_recon(s)
                 if 2 <= 4 * s + q < 6:
                     turn_x(4 * s + q + 2, "error")
-                if s in XSUM_STEPS and q == 1:
-                    sum_x(s)
                 if more_w and h == 0 and q in turn_after:
                     turn_w(k + 1, turn_after.index(q), "error")
                 if q == quant:
@@ -323,10 +308,10 @@ def tile_cssrclassifier_pa_kernel(tc, d_bytes, d_scale, W_dec, x, out_0, out_1, 
                         quantize_w(k + 1)
                     quantize_d(s + 1)
                 sum_max(s, q)
-                if s in XSUM_STEPS and q == 2:
-                    keep_xsum(s)
                 if 2 <= 4 * s + q < 6:
                     keep_x(4 * s + q + 2)
+                if 4 * s + q == 6:
+                    nc.vector.tensor_scalar(out=xsum01[:], in0=xsum[:], scalar1=-REDUCTION, scalar2=None, op0=ALU.mult)
                 if q == units_on_tensor(s) - 1:
                     sum_channels(s)
                 if q == quant and s + 2 < STEPS:

@@ -274,7 +274,7 @@ def tile_cssrclassifier_pa_kernel(tc, d_bytes, d_scale, W_dec, x, out_0, out_1, 
             k, h = divmod(s, 2)
             more_w = k + 1 < NCLS
             quant = 2 if s == 0 else 1
-            turn_after = (2, 3) if s == 0 else (0, 2)
+            turn_after = (2, 3) if s == 0 else (0, 3)
             if h == 0 and k + 3 < NCLS:
                 load_class(k + 3)
             for q in range(4):

@@ -318,22 +318,27 @@ def tile_cssrclassifier_pa_kernel(tc, d_bytes, d_scale, W_dec, x, out_0, out_1, 
                     interleave(s + 2, 0, "gpsimd")
                     interleave(s + 2, 1, "gpsimd")
 
-        for v in range(4):
-            mm_chsum(LAST, v)
-        for v in range(4):
-            part = work.tile([P, P], BF16, name="part", tag="part", bufs=2)
-            nc.scalar.activation(out=part[:], in_=chpart[LAST][:, v, :], func=ACT.Copy, accum_out=chsum[:, 4 * LAST + v:4 * LAST + v + 1])
         by_class = "p (k u) -> p k u"
         over_classes = "p (k u) -> p u k"
         linear = keep.tile([P, NCLS * UNITS], F32, name="linear")
-        nc.vector.scalar_tensor_tensor(
-            out=linear[:].rearrange(by_class, k=NCLS), in0=chsum[:].rearrange(by_class, k=NCLS), scalar=-REDUCTION,
-            in1=xsum01[:].rearrange("p (o u) -> p o u", o=1).to_broadcast([P, NCLS, UNITS]), op0=ALU.mult, op1=ALU.add,
-        )
         for q in range(4):
             mm_error(LAST, q)
+            if q == 1:
+                for v in range(4):
+                    mm_chsum(LAST, v)
             mm_recon(LAST, q)
             sum_max(LAST, q)
+            if q == 2:
+                nc.vector.scalar_tensor_tensor(
+                    out=linear[:].rearrange(by_class, k=NCLS), in0=chsum[:].rearrange(by_class, k=NCLS), scalar=-REDUCTION,
+                    in1=xsum01[:].rearrange("p (o u) -> p o u", o=1).to_broadcast([P, NCLS, UNITS]), op0=ALU.mult, op1=ALU.add,
+                )
+            if q == 1:
+                for v in range(4):
+                    part = work.tile([P, P], BF16, name="part", tag="part", bufs=2)
+                    nc.scalar.activation(
+                        out=part[:], in_=chpart[LAST][:, v, :], func=ACT.Copy, accum_out=chsum[:, 4 * LAST + v:4 * LAST + v + 1],
+                    )
             stage_recon(LAST, q)
             store_recon_part(LAST, q)
 

@@ -120,6 +120,8 @@ def tile_cssrclassifier_pa_kernel(tc, d_bytes, d_scale, W_dec, x, out_0, out_1, 
             dst = grouped[s][:, b2 * POS:(b2 + 1) * POS, :]
             src = wide[s][:, :, b2 * POS:(b2 + 1) * POS].rearrange("p t c -> p c t")
             if engine == "gpsimd":
+                dst = dst.rearrange("p (c i) t -> p c t i", i=4)
+                src = wide[s][:, :, b2 * POS:(b2 + 1) * POS].rearrange("p t (c i) -> p c t i", i=4)
                 nc.gpsimd.tensor_scalar(out=dst, in0=src, scalar1=1.0, scalar2=0.0, op0=ALU.mult, op1=ALU.add)
             else:
                 nc.vector.tensor_copy(out=dst, in_=src)

@@ -29,6 +29,7 @@ SPIN_FIRST = 7
 SPIN_BETWEEN = 2
 SCALAR_SUM_STEPS = [13, 14]
 SCALAR_UNITS = 2
+VECTOR_SUM_STEPS = [2, 4, 6, 8, 10, 12]
 
 
 def tile_cssrclassifier_pa_kernel(tc, d_bytes, d_scale, W_dec, x, out_0, out_1, out_2):
@@ -226,6 +227,8 @@ def tile_cssrclassifier_pa_kernel(tc, d_bytes, d_scale, W_dec, x, out_0, out_1, 
             )
 
         def units_on_tensor(s):
+            if s in VECTOR_SUM_STEPS:
+                return 3
             return 4 - SCALAR_UNITS if s in SCALAR_SUM_STEPS else 4
 
         def sum_channels(s):
@@ -295,7 +298,7 @@ def tile_cssrclassifier_pa_kernel(tc, d_bytes, d_scale, W_dec, x, out_0, out_1, 
                 if q >= 2 and s + 3 < STEPS:
                     widen(s + 3, q - 2, "scalar")
                 stage_recon(s, q)
-                if q >= units_on_tensor(s):
+                if q >= units_on_tensor(s) and s in SCALAR_SUM_STEPS:
                     sum_channels_scalar(s, q)
                 if q == 3:
                     store_recon(s)
@@ -310,6 +313,8 @@ def tile_cssrclassifier_pa_kernel(tc, d_bytes, d_scale, W_dec, x, out_0, out_1, 
                         quantize_w(k + 1)
                     quantize_d(s + 1)
                 sum_max(s, q)
+                if q >= units_on_tensor(s) and s in VECTOR_SUM_STEPS:
+                    nc.vector.tensor_reduce(out=chsum[:, 4 * s + q:4 * s + q + 1], in_=error[(s, q)][:], axis=AXIS.X, op=ALU.add)
                 if 2 <= 4 * s + q < 6:
                     keep_x(4 * s + q + 2)
                 if 4 * s + q == 6:

@@ -29,7 +29,8 @@ SPIN_FIRST = 7
 SPIN_BETWEEN = 2
 SCALAR_SUM_STEPS = [13, 14]
 SCALAR_UNITS = 2
-VECTOR_SUM_STEPS = [2, 4, 6, 8, 10, 12]
+VECTOR_SUM_STEPS = []
+DIRECT_STEPS = [2, 4, 6, 8, 10, 12]
 
 
 def tile_cssrclassifier_pa_kernel(tc, d_bytes, d_scale, W_dec, x, out_0, out_1, out_2):
@@ -101,13 +102,13 @@ def tile_cssrclassifier_pa_kernel(tc, d_bytes, d_scale, W_dec, x, out_0, out_1, 
 
         wide, grouped, dcodes, dscales = {}, {}, {}, {}
         wturned, wgrouped, wcodes, wscales = {}, {}, {}, {}
-        xturned, staged, recon, error, chpart = {}, {}, {}, {}, {}
+        xturned, staged, recon, error, chpart, diff = {}, {}, {}, {}, {}, {}
 
-        def widen(s, t, engine):
+        def widen(s, t, engine, images=(0, 1)):
             k, h = divmod(s, 2)
             if s not in wide:
-                wide[s] = work.tile([P, PACK, COLS], BF16, name="wide", tag="wide", bufs=3)
-            for b2 in range(2):
+                wide[s] = work.tile([P, PACK, COLS], BF16, name="wide", tag="wide", bufs=4)
+            for b2 in images:
                 src = dbytes[k][:, 2 * h + b2, t, :].bitcast(FP8)
                 dst = wide[s][:, t, b2 * POS:(b2 + 1) * POS]
                 if engine == "vector":
@@ -226,8 +227,17 @@ def tile_cssrclassifier_pa_kernel(tc, d_bytes, d_scale, W_dec, x, out_0, out_1, 
                 op0=ALU.mult, op1=ALU.max, accum_out=maxsum[:, 4 * s + v:4 * s + v + 1],
             )
 
+        def difference(s, v):
+            unit = 4 * (s % 2) + v
+            diff[(s, v)] = work.tile([P, CH], F32, name="diff", tag="diff", bufs=2)
+            nc.vector.tensor_tensor(out=diff[(s, v)][:], in0=error[(s, v)][:], in1=xT[:, unit, :], op=ALU.subtract)
+
+        def sum_abs(s, v):
+            halved = work.tile([P, CH], BF16, name="halved", tag="halved", bufs=2)
+            nc.scalar.activation(out=halved[:], in_=diff[(s, v)][:], func=ACT.Abs, scale=0.5, accum_out=maxsum[:, 4 * s + v:4 * s + v + 1])
+
         def units_on_tensor(s):
-            if s in VECTOR_SUM_STEPS:
+            if s in VECTOR_SUM_STEPS or s in DIRECT_STEPS:
                 return 3
             return 4 - SCALAR_UNITS if s in SCALAR_SUM_STEPS else 4
 
@@ -287,16 +297,25 @@ def tile_cssrclassifier_pa_kernel(tc, d_bytes, d_scale, W_dec, x, out_0, out_1, 
                 mm_error(s, q)
                 if q < units_on_tensor(s):
                     mm_chsum(s, q)
-                if q == h and s + 2 < STEPS:
+                direct, after_direct = s in DIRECT_STEPS, s - 1 in DIRECT_STEPS
+                if q == h and s + 2 < STEPS and not direct:
                     widen(s + 2, 2, "scalar")
+                if direct and q == 0 and s + 4 < STEPS:
+                    widen(s + 3, 0, "scalar", ())
+                    widen(s + 4, 0, "scalar")
                 if s == 0 and q == 1:
                     widen(2, 3, "scalar")
                 if more_w and h == 0 and q == turn_after[0] + 1:
                     group_w(k + 1, 0)
                 if more_w and h == 1 and q == 0:
                     group_w(k + 1, 1)
-                if q >= 2 and s + 3 < STEPS:
-                    widen(s + 3, q - 2, "scalar")
+                if after_direct:
+                    if q == 2 and s + 3 < STEPS:
+                        widen(s + 3, 1, "scalar")
+                    if q == 3:
+                        sum_abs(s - 1, 3)
+                elif q >= 2 and s + 3 < STEPS:
+                    widen(s + 3, q - 2, "scalar", (0,) if direct and q == 3 else (0, 1))
                 stage_recon(s, q)
                 if q >= units_on_tensor(s) and s in SCALAR_SUM_STEPS:
                     sum_channels_scalar(s, q)
@@ -309,16 +328,26 @@ def tile_cssrclassifier_pa_kernel(tc, d_bytes, d_scale, W_dec, x, out_0, out_1, 
                 if q == quant:
                     if s + 3 < STEPS:
                         widen(s + 3, 3, "vector")
+                    if direct:
+                        widen(s + 2, 2, "vector")
+                        widen(s + 3, 1, "vector", (1,))
                     if more_w and h == 1:
                         quantize_w(k + 1)
                     quantize_d(s + 1)
-                sum_max(s, q)
+                if direct and q == 3:
+                    difference(s, q)
+                else:
+                    sum_max(s, q)
                 if q >= units_on_tensor(s) and s in VECTOR_SUM_STEPS:
                     nc.vector.tensor_reduce(out=chsum[:, 4 * s + q:4 * s + q + 1], in_=error[(s, q)][:], axis=AXIS.X, op=ALU.add)
                 if 2 <= 4 * s + q < 6:
                     keep_x(4 * s + q + 2)
                 if 4 * s + q == 6:
                     nc.vector.tensor_scalar(out=xsum01[:], in0=xsum[:], scalar1=-REDUCTION, scalar2=None, op0=ALU.mult)
+                    nc.vector.tensor_scalar(
+                        out=chsum[:, 4 * DIRECT_STEPS[0] + 3:4 * DIRECT_STEPS[-1] + 4:8], in0=xsum[:, 3:4].to_broadcast([P, len(DIRECT_STEPS)]),
+                        scalar1=-1.0, scalar2=None, op0=ALU.mult,
+                    )
                 if q == units_on_tensor(s) - 1:
                     sum_channels(s)
                 if q == quant and s + 2 < STEPS:

@@ -316,6 +316,8 @@ def tile_cssrclassifier_pa_kernel(tc, d_bytes, d_scale, W_dec, x, out_0, out_1, 
                         sum_abs(s - 1, 3)
                 elif q >= 2 and s + 3 < STEPS:
                     widen(s + 3, q - 2, "scalar", (0,) if direct and q == 3 else (0, 1))
+                    if direct and q == 3 and s + 4 < STEPS:
+                        widen(s + 4, 3, "scalar", (0,))
                 stage_recon(s, q)
                 if q >= units_on_tensor(s) and s in SCALAR_SUM_STEPS:
                     sum_channels_scalar(s, q)
@@ -327,7 +329,7 @@ def tile_cssrclassifier_pa_kernel(tc, d_bytes, d_scale, W_dec, x, out_0, out_1, 
                     turn_w(k + 1, turn_after.index(q), "error")
                 if q == quant:
                     if s + 3 < STEPS:
-                        widen(s + 3, 3, "vector")
+                        widen(s + 3, 3, "vector", (1,) if after_direct else (0, 1))
                     if direct:
                         widen(s + 2, 2, "vector")
                         widen(s + 3, 1, "vector", (1,))

@@ -163,7 +163,7 @@ def tile_cssrclassifier_pa_kernel(tc, d_bytes, d_scale, W_dec, x, out_0, out_1, 
             b, f = divmod(u, 2)
             xturned[u] = bank([P, 4, P], BF16, "xturned", tag)
             for i in range(4):
-                nc.tensor.transpose(xturned[u][:, i, :], xraw[:, b, i, f * P:(f + 1) * P], ident_b[:])
+                nc.tensor.matmul(out=xturned[u][:, i, :], lhsT=xraw[:, b, i, f * P:(f + 1) * P], rhs=ident_b[:], start=True, stop=True)
 
         def keep_x(u):
             nc.vector.tensor_scalar(

@@ -82,9 +82,14 @@ def tile_cssrclassifier_pa_kernel(tc, d_bytes, d_scale, W_dec, x, out_0, out_1, 
 
         nc.sync.dma_start(out=scale[:], in_=d_scale[0, 0, :, 0, 0].rearrange("(p t) -> p t", t=PACK))
         load_d(0, 0, 2)
-        load_w(0)
+        for half in range(2):
+            nc.sync.dma_start(
+                out=wraw[0][:, 2 * half:2 * half + 2, :].rearrange("p i j -> p (i j)"),
+                in_=W_dec[0].rearrange("(m i) j -> m i j", i=4)[:, 2 * half:2 * half + 2, :].rearrange("m i j -> m (i j)"),
+            )
+        load_x(0, 1)
         load_d(0, 2, 4)
-        load_x(0, 2)
+        load_x(1, 2)
         load_d(1, 0, NIMG)
         load_x(2, 4)
         load_w(1)
@@ -269,17 +274,16 @@ def tile_cssrclassifier_pa_kernel(tc, d_bytes, d_scale, W_dec, x, out_0, out_1, 
         group_w(0, 1)
         widen(1, 0, "scalar")
         widen(1, 1, "scalar")
-        widen(1, 2, "vector")
-        widen(1, 3, "vector")
         quantize_w(0)
         quantize_d(0)
+        widen(1, 2, "vector")
+        widen(1, 3, "vector")
         interleave(1, 0, "gpsimd")
         interleave(1, 1, "gpsimd")
         turn_x(0, "error")
         turn_x(1, "error")
         turn_x(2, "error")
         turn_x(3, "chsum")
-        spin(SPIN_BETWEEN)
         for u in range(4):
             keep_x(u)
         widen(2, 0, "scalar")

from contextlib import ExitStack

import concourse.mybir as mybir
from concourse.masks import make_identity

F32 = mybir.dt.float32
BF16 = mybir.dt.bfloat16
U32 = mybir.dt.uint32
U8 = mybir.dt.uint8
FP8 = mybir.dt.float8_e4m3fn
FP8X4 = mybir.dt.float8_e4m3fn_x4
ALU = mybir.AluOpType
ACT = mybir.ActivationFunctionType
AXIS = mybir.AxisListType

NCLS, NIMG, CH, HID, POS = 8, 4, 512, 512, 256
P = 128
PACK = 4
STEPS = 2 * NCLS
LAST = STEPS - 1
COLS = 2 * POS
UNITS = 2 * NIMG
REDUCTION = -0.1
CLAMP = 500.0
FLOPS = 2 * NCLS * NIMG * CH * HID * POS

BANKS = {"recon": 2, "error": 4, "chsum": 2}
SPIN_FIRST = 7
SPIN_BETWEEN = 2
SCALAR_SUM_STEPS = [13, 14]
SCALAR_UNITS = 2
VECTOR_SUM_STEPS = []
DIRECT_STEPS = [2, 4, 6, 8, 10, 12]


def tile_cssrclassifier_pa_kernel(tc, d_bytes, d_scale, W_dec, x, out_0, out_1, out_2):
    nc = tc.nc
    with ExitStack() as ctx:
        keep = ctx.enter_context(tc.tile_pool(name="keep", bufs=1))
        work = ctx.enter_context(tc.tile_pool(name="work", bufs=2))
        psum = ctx.enter_context(tc.psum_pool(name="psum", bufs=2))
        ctx.enter_context(tc.manual_schedule())

        def bank(shape, dtype, name, tag):
            return psum.tile(shape, dtype, name=name, tag=tag, bufs=BANKS[tag])

        scale = keep.tile([P, PACK], F32, name="scale")
        dbytes = [keep.tile([P, NIMG, PACK, POS], U8, name="dbytes%d" % k) for k in range(NCLS)]
        wraw = [keep.tile([P, 4, HID], BF16, name="wraw%d" % k) for k in range(NCLS)]
        xraw = keep.tile([P, NIMG, 4, POS], BF16, name="xraw")
        xT = keep.tile([P, UNITS, CH], BF16, name="xT")
        ident_f = keep.tile([P, P], F32, name="ident_f")
        ident_b = keep.tile([P, P], BF16, name="ident_b")
        zero = keep.tile([P, 1], F32, name="zero")
        warm = keep.tile([P, 1], F32, name="warm")
        pick = keep.tile([P, NIMG, P], F32, name="pick")
        maxsum = keep.tile([P, NCLS * UNITS], F32, name="maxsum")
        chsum = keep.tile([P, NCLS * UNITS], F32, name="chsum")
        xsum = keep.tile([P, UNITS], F32, name="xsum")
        xsum01 = keep.tile([P, UNITS], F32, name="xsum01")
        pmat = keep.tile([P, P], F32, name="pmat")
        nothing = keep.tile([P, COLS], BF16, name="nothing")

        def load_d(k, b0, b1):
            nc.sync.dma_start(
                out=dbytes[k][:, b0:b1].rearrange("p b t n -> p b (t n)"),
                in_=d_bytes[k, b0:b1].rearrange("b (p t) y z -> p b (t y z)", t=PACK),
            )

        def load_w(k):
            nc.sync.dma_start(out=wraw[k][:].rearrange("p i j -> p (i j)"), in_=W_dec[k].rearrange("(m i) j -> m (i j)", i=4))

        def load_x(b0, b1):
            nc.sync.dma_start(
                out=xraw[:, b0:b1].rearrange("p b i n -> p b (i n)"),
                in_=x[b0:b1].rearrange("b (m i) y z -> m b (i y z)", i=4),
            )

        def load_class(k):
            load_d(k, 0, NIMG)
            load_w(k)

        nc.sync.dma_start(out=scale[:], in_=d_scale[0, 0, :, 0, 0].rearrange("(p t) -> p t", t=PACK))
        load_d(0, 0, 2)
        for half in range(2):
            nc.sync.dma_start(
                out=wraw[0][:, 2 * half:2 * half + 2, :].rearrange("p i j -> p (i j)"),
                in_=W_dec[0].rearrange("(m i) j -> m i j", i=4)[:, 2 * half:2 * half + 2, :].rearrange("m i j -> m (i j)"),
            )
        load_x(0, 1)
        load_d(0, 2, 4)
        load_x(1, 2)
        load_d(1, 0, NIMG)
        load_x(2, 4)
        load_w(1)
        load_class(2)

        nc.vector.memset(nothing[:], 0.0)
        nc.gpsimd.memset(zero[:], 0.0)
        make_identity(nc, ident_f[:])
        make_identity(nc, ident_b[:])
        nc.gpsimd.memset(pick[:], 0.0)
        for b in range(NIMG):
            nc.gpsimd.memset(pick[:, b, b:b + 1], 1.0 / POS)
        nc.gpsimd.memset(pmat[:], 0.0)
        nc.scalar.activation(out=warm[:], in_=zero[:], func=ACT.Exp)

        wide, grouped, dcodes, dscales = {}, {}, {}, {}
        wturned, wgrouped, wcodes, wscales = {}, {}, {}, {}
        xturned, staged, recon, error, chpart, diff = {}, {}, {}, {}, {}, {}

        def widen(s, t, engine, images=(0, 1)):
            k, h = divmod(s, 2)
            if s not in wide:
                wide[s] = work.tile([P, PACK, COLS], BF16, name="wide", tag="wide", bufs=4)
            for b2 in images:
                src = dbytes[k][:, 2 * h + b2, t, :].bitcast(FP8)
                dst = wide[s][:, t, b2 * POS:(b2 + 1) * POS]
                if engine == "vector":
                    nc.vector.tensor_scalar(out=dst, in0=src, scalar1=scale[:, t:t + 1], scalar2=None, op0=ALU.mult)
                else:
                    nc.scalar.activation(out=dst, in_=src, func=ACT.Copy, scale=scale[:, t:t + 1])

        def interleave(s, b2, engine):
            if b2 == 0:
                grouped[s] = work.tile([P, COLS, PACK], BF16, name="grouped", tag="grouped", bufs=1, align_bytes=64)
            dst = grouped[s][:, b2 * POS:(b2 + 1) * POS, :]
            src = wide[s][:, :, b2 * POS:(b2 + 1) * POS].rearrange("p t c -> p c t")
            if engine == "gpsimd":
                dst = dst.rearrange("p (c i) t -> p c t i", i=4)
                src = wide[s][:, :, b2 * POS:(b2 + 1) * POS].rearrange("p t (c i) -> p c t i", i=4)
                nc.gpsimd.tensor_scalar(out=dst, in0=src, scalar1=1.0, scalar2=0.0, op0=ALU.mult, op1=ALU.add)
            else:
                nc.vector.tensor_copy(out=dst, in_=src)

        def quantize_d(s):
            dcodes[s] = work.tile([P, COLS], U32, name="dcodes", tag="dcodes", bufs=3, align_bytes=64)
            dscales[s] = work.tile([P, COLS], U8, name="dscales", tag="dscales", bufs=3, align_bytes=64)
            nc.vector.quantize_mx(
                out=dcodes[s][:].bitcast(FP8X4), scales=dscales[s][:], in_=grouped[s][:].rearrange("p c t -> p (c t)"),
            )

        def turn_w(k, half, tag):
            tp = bank([P, 2, 2, P], F32, "wturned", tag)
            wturned[(k, half)] = tp
            for i2 in range(2):
                words = wraw[k][:, 2 * half + i2, :].bitcast(F32)
                for u in range(2):
                    nc.tensor.transpose(tp[:, i2, u, :], words[:, u:HID // 2:2], ident_f[:])

        def group_w(k, half):
            if half == 0:
                wgrouped[k] = work.tile([P, CH, PACK], BF16, name="wgrouped", tag="wgrouped", bufs=2, align_bytes=64)
            words = wgrouped[k][:].rearrange("p c t -> p (c t)").bitcast(F32)
            nc.scalar.copy(
                out=words[:, half * CH:(half + 1) * CH].rearrange("p (i m u) -> p i m u", i=2, u=2),
                in_=wturned[(k, half)][:].rearrange("p i u m -> p i m u"),
            )

        def quantize_w(k):
            wcodes[k] = work.tile([P, CH], U32, name="wcodes", tag="wcodes", bufs=2, align_bytes=64)
            wscales[k] = work.tile([P, CH], U8, name="wscales", tag="wscales", bufs=2, align_bytes=64)
            nc.vector.quantize_mx(
                out=wcodes[k][:].bitcast(FP8X4), scales=wscales[k][:], in_=wgrouped[k][:].rearrange("p c t -> p (c t)"),
            )

        def turn_x(u, tag):
            b, f = divmod(u, 2)
            xturned[u] = bank([P, 4, P], BF16, "xturned", tag)
            for i in range(4):
                nc.tensor.matmul(out=xturned[u][:, i, :], lhsT=xraw[:, b, i, f * P:(f + 1) * P], rhs=ident_b[:], start=True, stop=True)

        def keep_x(u):
            nc.vector.tensor_scalar(
                out=xT[:, u, :], in0=xturned[u][:].rearrange("p i m -> p (i m)"), scalar1=1.0, scalar2=None,
                op0=ALU.mult, op1=ALU.add, accum_out=xsum[:, u:u + 1],
            )

        def mm_recon(s, i):
            k = s // 2
            recon[(s, i)] = bank([P, COLS], F32, "recon", "recon")
            cols = slice(i * P, (i + 1) * P)
            nc.tensor.matmul_mx(
                out=recon[(s, i)][:], lhsT=wcodes[k][:, cols].bitcast(FP8X4), lhsT_scale=wscales[k][:, cols],
                rhs=dcodes[s][:].bitcast(FP8X4), rhs_scale=dscales[s][:], start=True, stop=True,
            )

        def stage_recon(s, i):
            if i == 0:
                staged[s] = work.tile([P, 2, 4, POS], F32, name="staged", tag="staged", bufs=3)
            nc.scalar.copy(out=staged[s][:, :, i, :], in_=recon[(s, i)][:].rearrange("p (b n) -> p b n", b=2))

        def store_recon(s):
            k, h = divmod(s, 2)
            nc.sync.dma_start(
                out=out_2[2 * h:2 * h + 2, k].rearrange("b (m i) y z -> m b (i y z)", i=4),
                in_=staged[s][:].rearrange("p b i n -> p b (i n)"),
            )

        def store_recon_part(s, i):
            k, h = divmod(s, 2)
            nc.sync.dma_start(
                out=out_2[2 * h:2 * h + 2, k].rearrange("b (m i) y z -> i m b (y z)", i=4)[i], in_=staged[s][:, :, i, :],
            )

        def mm_error(s, v):
            k = s // 2
            error[(s, v)] = bank([P, CH], F32, "error", "error")
            cols = slice(v * P, (v + 1) * P)
            nc.tensor.matmul_mx(
                out=error[(s, v)][:], lhsT=dcodes[s][:, cols].bitcast(FP8X4), lhsT_scale=dscales[s][:, cols],
                rhs=wcodes[k][:].bitcast(FP8X4), rhs_scale=wscales[k][:], start=True, stop=True,
            )

        def mm_chsum(s, v):
            k = s // 2
            if v == 0:
                chpart[s] = bank([P, 4, P], F32, "chpart", "chsum")
            cols = slice(v * P, (v + 1) * P)
            for i in range(4):
                group = slice(i * P, (i + 1) * P)
                nc.tensor.matmul_mx(
                    out=chpart[s][:, v, :], lhsT=dcodes[s][:, cols].bitcast(FP8X4), lhsT_scale=dscales[s][:, cols],
                    rhs=wcodes[k][:, group].bitcast(FP8X4), rhs_scale=wscales[k][:, group], start=(i == 0), stop=(i == 3),
                )

        def sum_max(s, v):
            unit = 4 * (s % 2) + v
            maxima = work.tile([P, CH], F32, name="maxima", tag="maxima", bufs=2)
            nc.vector.scalar_tensor_tensor(
                out=maxima[:], in0=error[(s, v)][:], scalar=1.0, in1=xT[:, unit, :],
                op0=ALU.mult, op1=ALU.max, accum_out=maxsum[:, 4 * s + v:4 * s + v + 1],
            )

        def difference(s, v):
            unit = 4 * (s % 2) + v
            diff[(s, v)] = work.tile([P, CH], F32, name="diff", tag="diff", bufs=2)
            nc.vector.tensor_tensor(out=diff[(s, v)][:], in0=error[(s, v)][:], in1=xT[:, unit, :], op=ALU.subtract)

        def sum_abs(s, v):
            halved = work.tile([P, CH], BF16, name="halved", tag="halved", bufs=2)
            nc.scalar.activation(out=halved[:], in_=diff[(s, v)][:], func=ACT.Abs, scale=0.5, accum_out=maxsum[:, 4 * s + v:4 * s + v + 1])

        def units_on_tensor(s):
            if s in VECTOR_SUM_STEPS or s in DIRECT_STEPS:
                return 3
            return 4 - SCALAR_UNITS if s in SCALAR_SUM_STEPS else 4

        def sum_channels(s):
            n = units_on_tensor(s)
            nc.vector.tensor_reduce(out=chsum[:, 4 * s:4 * s + n], in_=chpart[s][:, 0:n, :], axis=AXIS.X, op=ALU.add)

        def sum_channels_scalar(s, v):
            copied = work.tile([P, CH], F32, name="copied", tag="copied", bufs=2)
            nc.scalar.activation(out=copied[:], in_=error[(s, v)][:], func=ACT.Copy, accum_out=chsum[:, 4 * s + v:4 * s + v + 1])

        unread = bank([P, COLS], F32, "unread", "chsum")

        def spin(count):
            for n in range(count):
                nc.tensor.matmul(out=unread[:], lhsT=nothing[:, 0:P], rhs=nothing[:], start=True, stop=True)

        spin(SPIN_FIRST)
        widen(0, 0, "scalar")
        widen(0, 1, "scalar")
        widen(0, 2, "vector")
        widen(0, 3, "vector")
        turn_w(0, 0, "error")
        turn_w(0, 1, "recon")
        spin(SPIN_BETWEEN)
        interleave(0, 0, "vector")
        interleave(0, 1, "vector")
        group_w(0, 0)
        group_w(0, 1)
        widen(1, 0, "scalar")
        widen(1, 1, "scalar")
        quantize_w(0)
        quantize_d(0)
        widen(1, 2, "vector")
        widen(1, 3, "vector")
        interleave(1, 0, "gpsimd")
        interleave(1, 1, "gpsimd")
        turn_x(0, "error")
        turn_x(1, "error")
        turn_x(2, "error")
        turn_x(3, "chsum")
        for u in range(4):
            keep_x(u)
        widen(2, 0, "scalar")
        widen(2, 1, "scalar")

        for s in range(LAST):
            k, h = divmod(s, 2)
            more_w = k + 1 < NCLS
            quant = 2 if s == 0 else 1
            turn_after = (2, 3) if s == 0 else (0, 3)
            if h == 0 and k + 3 < NCLS:
                load_class(k + 3)
            for q in range(4):
                mm_recon(s, q)
                mm_error(s, q)
                if q < units_on_tensor(s):
                    mm_chsum(s, q)
                direct, after_direct = s in DIRECT_STEPS, s - 1 in DIRECT_STEPS
                if q == h and s + 2 < STEPS and not direct:
                    widen(s + 2, 2, "scalar")
                if direct and q == 0 and s + 4 < STEPS:
                    widen(s + 3, 0, "scalar", ())
                    widen(s + 4, 0, "scalar")
                if s == 0 and q == 1:
                    widen(2, 3, "scalar")
                if more_w and h == 0 and q == turn_after[0] + 1:
                    group_w(k + 1, 0)
                if more_w and h == 1 and q == 0:
                    group_w(k + 1, 1)
                if after_direct:
                    if q == 2 and s + 3 < STEPS:
                        widen(s + 3, 1, "scalar")
                    if q == 3:
                        sum_abs(s - 1, 3)
                elif q >= 2 and s + 3 < STEPS:
                    widen(s + 3, q - 2, "scalar", (0,) if direct and q == 3 else (0, 1))
                    if direct and q == 3 and s + 4 < STEPS:
                        widen(s + 4, 3, "scalar", (0,))
                stage_recon(s, q)
                if q >= units_on_tensor(s) and s in SCALAR_SUM_STEPS:
                    sum_channels_scalar(s, q)
                if q == 3:
                    store_recon(s)
                if 2 <= 4 * s + q < 6:
                    turn_x(4 * s + q + 2, "error")
                if more_w and h == 0 and q in turn_after:
                    turn_w(k + 1, turn_after.index(q), "error")
                if q == quant:
                    if s + 3 < STEPS:
                        widen(s + 3, 3, "vector", (1,) if after_direct else (0, 1))
                    if direct:
                        widen(s + 2, 2, "vector")
                        widen(s + 3, 1, "vector", (1,))
                    if more_w and h == 1:
                        quantize_w(k + 1)
                    quantize_d(s + 1)
                if direct and q == 3:
                    difference(s, q)
                else:
                    sum_max(s, q)
                if q >= units_on_tensor(s) and s in VECTOR_SUM_STEPS:
                    nc.vector.tensor_reduce(out=chsum[:, 4 * s + q:4 * s + q + 1], in_=error[(s, q)][:], axis=AXIS.X, op=ALU.add)
                if 2 <= 4 * s + q < 6:
                    keep_x(4 * s + q + 2)
                if 4 * s + q == 6:
                    nc.vector.tensor_scalar(out=xsum01[:], in0=xsum[:], scalar1=-REDUCTION, scalar2=None, op0=ALU.mult)
                    nc.vector.tensor_scalar(
                        out=chsum[:, 4 * DIRECT_STEPS[0] + 3:4 * DIRECT_STEPS[-1] + 4:8], in0=xsum[:, 3:4].to_broadcast([P, len(DIRECT_STEPS)]),
                        scalar1=-1.0, scalar2=None, op0=ALU.mult,
                    )
                if q == units_on_tensor(s) - 1:
                    sum_channels(s)
                if q == quant and s + 2 < STEPS:
                    interleave(s + 2, 0, "gpsimd")
                    interleave(s + 2, 1, "gpsimd")

        by_class = "p (k u) -> p k u"
        over_classes = "p (k u) -> p u k"
        linear = keep.tile([P, NCLS * UNITS], F32, name="linear")
        for q in range(4):
            mm_error(LAST, q)
            if q == 1:
                for v in range(4):
                    mm_chsum(LAST, v)
            mm_recon(LAST, q)
            sum_max(LAST, q)
            if q == 2:
                nc.vector.scalar_tensor_tensor(
                    out=linear[:].rearrange(by_class, k=NCLS), in0=chsum[:].rearrange(by_class, k=NCLS), scalar=-REDUCTION,
                    in1=xsum01[:].rearrange("p (o u) -> p o u", o=1).to_broadcast([P, NCLS, UNITS]), op0=ALU.mult, op1=ALU.add,
                )
            if q == 1:
                for v in range(4):
                    part = work.tile([P, P], BF16, name="part", tag="part", bufs=2)
                    nc.scalar.activation(
                        out=part[:], in_=chpart[LAST][:, v, :], func=ACT.Copy, accum_out=chsum[:, 4 * LAST + v:4 * LAST + v + 1],
                    )
            stage_recon(LAST, q)
            store_recon_part(LAST, q)

        raw = keep.tile([P, NCLS * UNITS], F32, name="raw")
        nc.vector.scalar_tensor_tensor(out=raw[:], in0=maxsum[:], scalar=2.0 * REDUCTION, in1=linear[:], op0=ALU.mult, op1=ALU.add)
        logits = keep.tile([P, NCLS * UNITS], F32, name="logits")
        nc.vector.tensor_scalar(out=logits[:], in0=raw[:], scalar1=-CLAMP, scalar2=CLAMP, op0=ALU.max, op1=ALU.min)
        halves = keep.tile([P, NIMG * NCLS], F32, name="halves")
        split = logits[:].rearrange("p (k b f) -> p k b f", k=NCLS, b=NIMG)
        nc.vector.tensor_tensor(
            out=halves[:].rearrange("p (b k) -> p k b", b=NIMG), in0=split[:, :, :, 0], in1=split[:, :, :, 1], op=ALU.add,
        )
        top = keep.tile([P, UNITS], F32, name="top")
        nc.vector.tensor_reduce(out=top[:], in_=logits[:].rearrange(over_classes, k=NCLS), axis=AXIS.X, op=ALU.max)
        shifted = keep.tile([P, NCLS * UNITS], F32, name="shifted")
        nc.vector.tensor_tensor(
            out=shifted[:].rearrange(by_class, k=NCLS), in0=logits[:].rearrange(by_class, k=NCLS),
            in1=top[:].rearrange("p (o u) -> p o u", o=1).to_broadcast([P, NCLS, UNITS]), op=ALU.subtract,
        )
        expd = keep.tile([P, NCLS * UNITS], F32, name="expd")
        nc.scalar.activation(out=expd[:], in_=shifted[:], func=ACT.Exp)

        pooled = bank([P, NCLS], F32, "pooled", "chsum")
        for b in range(NIMG):
            nc.tensor.matmul(
                out=pooled[:], lhsT=pick[:, b, :], rhs=halves[:, b * NCLS:(b + 1) * NCLS], start=(b == 0), stop=(b == NIMG - 1),
            )
        pooled_sb = keep.tile([P, NCLS], F32, name="pooled_sb")
        nc.scalar.copy(out=pooled_sb[:], in_=pooled[:])
        nc.sync.dma_start(out=out_1, in_=pooled_sb[0:NIMG, :])

        total = keep.tile([P, UNITS], F32, name="total")
        nc.vector.tensor_reduce(out=total[:], in_=expd[:].rearrange(over_classes, k=NCLS), axis=AXIS.X, op=ALU.add)
        inverse = keep.tile([P, UNITS], F32, name="inverse")
        nc.vector.reciprocal(out=inverse[:], in_=total[:])
        nc.vector.tensor_tensor(
            out=pmat[:, 0:NCLS * UNITS].rearrange("p (b k f) -> p k b f", b=NIMG, k=NCLS),
            in0=expd[:].rearrange("p (k b f) -> p k b f", k=NCLS, b=NIMG),
            in1=inverse[:].rearrange("p (o b f) -> p o b f", o=1, b=NIMG).to_broadcast([P, NCLS, NIMG, 2]), op=ALU.mult,
        )
        pturned = bank([P, P], F32, "pturned", "recon")
        nc.tensor.transpose(pturned[:], pmat[:], ident_f[:])
        prows = keep.tile([P, P], F32, name="prows")
        nc.vector.tensor_copy(out=prows[:], in_=pturned[:])
        nc.sync.dma_start(out=out_0.rearrange("b k (f g) w -> (b k f) (g w)", f=2), in_=prows[0:NCLS * UNITS, :])
